import numpy as np
import ml_dtypes


def mxq(x, axis, fmt="e4m3"):
    dtype, down = {"e4m3": (ml_dtypes.float8_e4m3fn, 7), "e5m2": (ml_dtypes.float8_e5m2, 14)}[fmt]
    v = np.moveaxis(np.asarray(x, np.float32).astype(ml_dtypes.bfloat16).astype(np.float64), axis, -1)
    blocks = v.reshape(v.shape[:-1] + (-1, 32))
    amax = np.abs(blocks).max(-1, keepdims=True)
    byte = np.maximum(np.where(amax > 0, np.frexp(amax)[1] - 1 + 127, 0) - down, 1)
    scale = np.exp2(byte - 127.0)
    codes = (blocks / scale).astype(np.float32).astype(dtype).astype(np.float64)
    return np.moveaxis((codes * scale).reshape(v.shape), -1, axis)


WIDE = False


def mx_kscale(k):
    if not WIDE:
        return np.ones(k)
    levels = np.array([10, -10, 5, -5, 0])
    a = np.random.permutation(np.resize(levels, k // 512 * 4)).reshape(k // 512, 4)
    idx = np.arange(k)
    return np.exp2(a[idx // 512, idx % 128 // 32])


BF16 = ml_dtypes.bfloat16


def bf(x):
    return np.asarray(x, np.float32).astype(BF16)


def f64(x):
    return np.asarray(x).astype(np.float64)


B, T, V, C, K, R = 2, 4, 16, 512, 512, 256


def setup_inputs():
    n = np.random.standard_normal
    s = mx_kscale(C)
    x = 0.7 * n((B, 1, V, C)) + 0.7 * n((B, T, V, C))
    return {
        "x": bf(x * s),
        "A": bf(np.eye(V) + 0.1 * n((K, V, V))),
        "lam": bf(0.25 + 0.1 * np.random.random(1)),
        "phi_w": bf(n((C, K)) / np.sqrt(C) / s[:, None]),
        "phi_b": bf(0.3 * n(K)),
        "theta_w": bf(n((C, K)) / np.sqrt(C) / s[:, None]),
        "theta_b": bf(0.3 * n(K)),
        "kappa_w": bf(n((K, K)) / np.sqrt(K)),
        "kappa_b": bf(0.3 * n(K)),
    }


def reference(x, A, lam, phi_w, phi_b, theta_w, theta_b, kappa_w, kappa_b):
    xq = mxq(f64(x), 3, "e4m3")
    phi_x = ((xq @ mxq(f64(phi_w), 0, "e4m3")) + f64(phi_b)).mean(axis=1)
    theta_x = ((xq @ mxq(f64(theta_w), 0, "e4m3")) + f64(theta_b)).mean(axis=1)
    F_ij = np.tanh(phi_x[:, :, None, :] - theta_x[:, None, :, :])
    A_hat = np.transpose((mxq(F_ij, 3, "e4m3") @ mxq(f64(kappa_w), 0, "e4m3")) + f64(kappa_b), (0, 3, 1, 2))
    return f64(A)[None] + f64(lam) * A_hat

@@ -1,0 +1,205 @@
+from contextlib import ExitStack
+
+import concourse.mybir as mybir
+from concourse.masks import make_identity
+
+F32 = mybir.dt.float32
+BF16 = mybir.dt.bfloat16
+U32 = mybir.dt.uint32
+U8 = mybir.dt.uint8
+FP8X4 = mybir.dt.float8_e4m3fn_x4
+ALU = mybir.AluOpType
+ACT = mybir.ActivationFunctionType
+
+P = 128
+PACK = 4
+B, T, V, C = 2, 4, 16, 512
+ROWS = B * T * V
+PAIRS = V * V
+U_PIECE = 8
+VECTOR_GROUPS = 84
+
+FLOPS = 2 * ROWS * C * C * 2 + 2 * B * PAIRS * C * C
+
+
+def load_weight(nc, pool, w, name):
+    raw = pool.tile([P, PACK, C], BF16, name=name + "_raw")
+    nc.sync.dma_start(out=raw[:], in_=w.rearrange("(p j) c -> p j c", j=PACK))
+    return raw
+
+
+def regroup_weight(nc, pool, raw, name, vector_groups):
+    grouped = pool.tile([P, PACK * C], BF16, name=name + "_grouped", align_bytes=64)
+    dst = grouped[:].rearrange("p (t q j) -> p q j t", t=PACK, j=PACK)
+    src = raw[:].rearrange("p j (q t) -> p q j t", t=PACK)
+    if vector_groups > 0:
+        nc.vector.tensor_copy(out=dst[:, 0:vector_groups], in_=src[:, 0:vector_groups])
+    nc.scalar.copy(out=dst[:, vector_groups:P], in_=src[:, vector_groups:P])
+    return grouped
+
+
+def quantise_weight(nc, pool, grouped, name):
+    codes = pool.tile([P, C], U32, name=name + "_codes", align_bytes=64)
+    scales = pool.tile([P, C], U8, name=name + "_scales", align_bytes=64)
+    nc.vector.quantize_mx(out=codes[:].bitcast(FP8X4), scales=scales[:], in_=grouped[:])
+    return codes, scales
+
+
+def tile_attgcn_pa_s_kernel(
+    tc, x, A, lam, phi_w, phi_b, theta_w, theta_b, kappa_w, kappa_b, out
+):
+    nc = tc.nc
+    with ExitStack() as ctx:
+        keep = ctx.enter_context(tc.tile_pool(name="keep", bufs=1))
+        psum = ctx.enter_context(tc.psum_pool(name="psum", bufs=1))
+
+        x_sb = keep.tile([P, C], BF16)
+        nc.sync.dma_start(out=x_sb[:], in_=x.rearrange("b s v f -> (b s v) f"))
+        phi_raw = load_weight(nc, keep, phi_w, "phi")
+        theta_raw = load_weight(nc, keep, theta_w, "theta")
+        kappa_raw = load_weight(nc, keep, kappa_w, "kappa")
+        a_bf = keep.tile([P, PACK, PAIRS], BF16)
+        nc.sync.dma_start(out=a_bf[:], in_=A.rearrange("(q m) u v -> q m (u v)", m=PACK))
+
+        phi_b_bf = keep.tile([P, PACK], BF16)
+        nc.scalar.dma_start(out=phi_b_bf[:], in_=phi_b.rearrange("(q t) -> q t", t=PACK))
+        theta_b_bf = keep.tile([P, PACK], BF16)
+        nc.scalar.dma_start(out=theta_b_bf[:], in_=theta_b.rearrange("(q t) -> q t", t=PACK))
+        kappa_b_bf = keep.tile([P, PACK], BF16)
+        nc.scalar.dma_start(out=kappa_b_bf[:], in_=kappa_b.rearrange("(q m) -> q m", m=PACK))
+        lam_bf = keep.tile([P, 1], BF16)
+        nc.scalar.dma_start(out=lam_bf[:], in_=lam.partition_broadcast(P))
+
+        warm_in = keep.tile([P, 1], F32)
+        nc.vector.memset(warm_in[:], 0.0)
+        warm_out = keep.tile([P, 1], F32)
+        nc.scalar.activation(out=warm_out[:], in_=warm_in[:], func=ACT.Tanh)
+
+        ident = keep.tile([P, P], F32)
+        make_identity(nc, ident[:])
+
+        bias_diff = keep.tile([P, PACK], F32)
+        nc.gpsimd.tensor_tensor(out=bias_diff[:], in0=phi_b_bf[:], in1=theta_b_bf[:], op=ALU.subtract)
+        lam_f = keep.tile([P, 1], F32)
+        nc.gpsimd.tensor_copy(out=lam_f[:], in_=lam_bf[:])
+        lam_kappa_b = keep.tile([P, PACK], F32)
+        nc.gpsimd.tensor_scalar(
+            out=lam_kappa_b[:], in0=kappa_b_bf[:], scalar1=lam_f[:, 0:1], scalar2=None, op0=ALU.mult
+        )
+
+        x_words = x_sb[:].bitcast(F32).rearrange("r (q h) -> r h q", h=2)
+        x_t = psum.tile([P, 2, ROWS], F32, tag="bank7")
+        for h in range(2):
+            nc.tensor.transpose(x_t[:, h, :], x_words[:, h, :], ident[:])
+        x_grouped = keep.tile([P, ROWS * PACK], BF16, align_bytes=64)
+        x_dst = x_grouped[:].bitcast(F32).rearrange("q (b v s h) -> q b v s h", b=B, v=V, s=T)
+        x_src = x_t[:].rearrange("q h (b s v) -> q b v s h", b=B, s=T)
+        for b in range(B):
+            nc.vector.tensor_copy(out=x_dst[:, b], in_=x_src[:, b])
+        x_codes = keep.tile([P, ROWS], U32, align_bytes=64)
+        x_scales = keep.tile([P, ROWS], U8, align_bytes=64)
+        nc.vector.quantize_mx(out=x_codes[:].bitcast(FP8X4), scales=x_scales[:], in_=x_grouped[:])
+
+        def project(raw, name, bank):
+            grouped = regroup_weight(nc, keep, raw, name, VECTOR_GROUPS)
+            codes, scales = quantise_weight(nc, keep, grouped, name)
+            acc = psum.tile([P, PACK, ROWS], F32, tag=bank, name=name + "_acc")
+            for t in range(PACK):
+                cols = slice(t * P, (t + 1) * P)
+                nc.tensor.matmul_mx(
+                    out=acc[:, t, :],
+                    lhsT=codes[:, cols].bitcast(FP8X4),
+                    lhsT_scale=scales[:, cols],
+                    rhs=x_codes[:].bitcast(FP8X4),
+                    rhs_scale=x_scales[:],
+                    start=True,
+                    stop=True,
+                )
+            return acc
+
+        def sum_over_time(acc, name):
+            total = keep.tile([P, B, V, PACK], F32, name=name + "_sum")
+            nc.vector.tensor_reduce(
+                out=total[:].rearrange("q b v t -> q (b v) t"),
+                in_=acc[:].rearrange("q t (n s) -> q n t s", s=T),
+                axis=mybir.AxisListType.X,
+                op=ALU.add,
+            )
+            return total
+
+        phi_acc = project(phi_raw, "phi", "bank5")
+        theta_acc = project(theta_raw, "theta", "bank6")
+        kappa_grouped = regroup_weight(nc, keep, kappa_raw, "kappa", 0)
+
+        phi_sum = sum_over_time(phi_acc, "phi")
+        phi_biased = keep.tile([P, B, V, PACK], F32)
+        nc.vector.scalar_tensor_tensor(
+            out=phi_biased[:].rearrange("q b v t -> q (b v) t"),
+            in0=bias_diff[:].unsqueeze(1).to_broadcast([P, B * V, PACK]),
+            scalar=float(T),
+            in1=phi_sum[:].rearrange("q b v t -> q (b v) t"),
+            op0=ALU.mult,
+            op1=ALU.add,
+        )
+        theta_sum = sum_over_time(theta_acc, "theta")
+
+        a_plus = keep.tile([P, PACK, PAIRS], F32)
+        for m in range(PACK):
+            nc.scalar.activation(
+                out=a_plus[:, m, :], in_=a_bf[:, m, :], func=ACT.Identity, bias=lam_kappa_b[:, m : m + 1]
+            )
+
+        diff = keep.tile([P, B, V, V, PACK], F32)
+        f_bf = keep.tile([P, B, V, V, PACK], BF16, align_bytes=64)
+        for b in range(B):
+            for u0 in range(0, V, U_PIECE):
+                us = slice(u0, u0 + U_PIECE)
+                nc.vector.tensor_tensor(
+                    out=diff[:, b, us],
+                    in0=phi_biased[:, b, us, :].unsqueeze(2).to_broadcast([P, U_PIECE, V, PACK]),
+                    in1=theta_sum[:, b].unsqueeze(1).to_broadcast([P, U_PIECE, V, PACK]),
+                    op=ALU.subtract,
+                )
+                nc.scalar.activation(
+                    out=f_bf[:, b, us].rearrange("q u v t -> q (u v t)"),
+                    in_=diff[:, b, us].rearrange("q u v t -> q (u v t)"),
+                    func=ACT.Tanh,
+                    scale=1.0 / T,
+                )
+
+        kappa_codes, kappa_scales = quantise_weight(nc, keep, kappa_grouped, "kappa")
+
+        f_codes = keep.tile([P, B, PAIRS], U32, align_bytes=64)
+        f_scales = keep.tile([P, B, PAIRS], U8, align_bytes=64)
+        out_sb = keep.tile([P, B, PACK, PAIRS], F32)
+        out_view = out.rearrange("b (q m) u v -> b q m (u v)", m=PACK)
+        for b in range(B):
+            nc.vector.quantize_mx(
+                out=f_codes[:, b, :].bitcast(FP8X4),
+                scales=f_scales[:, b, :],
+                in_=f_bf[:, b].rearrange("q u v t -> q (u v t)"),
+            )
+        for b in range(B):
+            for m in range(PACK):
+                cols = slice(m * P, (m + 1) * P)
+                g = psum.tile([P, PAIRS], F32, tag="bank%d" % (b * PACK + m), name="g%d%d" % (b, m))
+                nc.tensor.matmul_mx(
+                    out=g[:],
+                    lhsT=kappa_codes[:, cols].bitcast(FP8X4),
+                    lhsT_scale=kappa_scales[:, cols],
+                    rhs=f_codes[:, b, :].bitcast(FP8X4),
+                    rhs_scale=f_scales[:, b, :],
+                    start=True,
+                    stop=True,
+                )
+                nc.vector.scalar_tensor_tensor(
+                    out=out_sb[:, b, m, :],
+                    in0=g[:],
+                    scalar=lam_f[:, 0:1],
+                    in1=a_plus[:, m, :],
+                    op0=ALU.mult,
+                    op1=ALU.add,
+                )
+                if m % 2 == 1:
+                    ms = slice(m - 1, m + 1)
+                    nc.sync.dma_start(out=out_view[b, :, ms, :], in_=out_sb[:, b, ms, :])

@@ -52,6 +52,7 @@ def tile_attgcn_pa_s_kernel(
     with ExitStack() as ctx:
         keep = ctx.enter_context(tc.tile_pool(name="keep", bufs=1))
         psum = ctx.enter_context(tc.psum_pool(name="psum", bufs=1))
+        ctx.enter_context(tc.manual_schedule())
 
         x_sb = keep.tile([P, C], BF16)
         nc.sync.dma_start(out=x_sb[:], in_=x.rearrange("b s v f -> (b s v) f"))
@@ -143,12 +144,6 @@ def tile_attgcn_pa_s_kernel(
         )
         theta_sum = sum_over_time(theta_acc, "theta")
 
-        a_plus = keep.tile([P, PACK, PAIRS], F32)
-        for m in range(PACK):
-            nc.scalar.activation(
-                out=a_plus[:, m, :], in_=a_bf[:, m, :], func=ACT.Identity, bias=lam_kappa_b[:, m : m + 1]
-            )
-
         diff = keep.tile([P, B, V, V, PACK], F32)
         f_bf = keep.tile([P, B, V, V, PACK], BF16, align_bytes=64)
         for b in range(B):
@@ -179,6 +174,12 @@ def tile_attgcn_pa_s_kernel(
                 scales=f_scales[:, b, :],
                 in_=f_bf[:, b].rearrange("q u v t -> q (u v t)"),
             )
+        a_plus = keep.tile([P, PACK, PAIRS], F32)
+        for m in range(PACK):
+            nc.scalar.activation(
+                out=a_plus[:, m, :], in_=a_bf[:, m, :], func=ACT.Identity, bias=lam_kappa_b[:, m : m + 1]
+            )
+
         for b in range(B):
             for m in range(PACK):
                 cols = slice(m * P, (m + 1) * P)
@@ -200,6 +201,4 @@ def tile_attgcn_pa_s_kernel(
                     op0=ALU.mult,
                     op1=ALU.add,
                 )
-                if m % 2 == 1:
-                    ms = slice(m - 1, m + 1)
-                    nc.sync.dma_start(out=out_view[b, :, ms, :], in_=out_sb[:, b, ms, :])
+                nc.sync.dma_start(out=out_view[b, :, m, :], in_=out_sb[:, b, m, :])

@@ -7,6 +7,7 @@ F32 = mybir.dt.float32
 BF16 = mybir.dt.bfloat16
 U32 = mybir.dt.uint32
 U8 = mybir.dt.uint8
+I32 = mybir.dt.int32
 FP8X4 = mybir.dt.float8_e4m3fn_x4
 ALU = mybir.AluOpType
 ACT = mybir.ActivationFunctionType
@@ -15,9 +16,12 @@ P = 128
 PACK = 4
 B, T, V, C = 2, 4, 16, 512
 ROWS = B * T * V
+POSES = B * V
 PAIRS = V * V
+N_MIN = 128
 U_PIECE = 8
 VECTOR_GROUPS = 84
+KAPPA_VECTOR_GROUPS = P - VECTOR_GROUPS
 
 FLOPS = 2 * ROWS * C * C * 2 + 2 * B * PAIRS * C * C
 
@@ -32,16 +36,20 @@ def regroup_weight(nc, pool, raw, name, vector_groups):
     grouped = pool.tile([P, PACK * C], BF16, name=name + "_grouped", align_bytes=64)
     dst = grouped[:].rearrange("p (t q j) -> p q j t", t=PACK, j=PACK)
     src = raw[:].rearrange("p j (q t) -> p q j t", t=PACK)
-    if vector_groups > 0:
-        nc.vector.tensor_copy(out=dst[:, 0:vector_groups], in_=src[:, 0:vector_groups])
+    nc.vector.tensor_copy(out=dst[:, 0:vector_groups], in_=src[:, 0:vector_groups])
     nc.scalar.copy(out=dst[:, vector_groups:P], in_=src[:, vector_groups:P])
     return grouped
 
 
 def quantise_weight(nc, pool, grouped, name):
-    codes = pool.tile([P, C], U32, name=name + "_codes", align_bytes=64)
-    scales = pool.tile([P, C], U8, name=name + "_scales", align_bytes=64)
-    nc.vector.quantize_mx(out=codes[:].bitcast(FP8X4), scales=scales[:], in_=grouped[:])
+    codes = pool.tile([P, PACK, P], U32, name=name + "_codes", align_bytes=64)
+    scales = pool.tile([P, PACK, P], U8, name=name + "_scales", align_bytes=64)
+    for t in range(PACK):
+        nc.vector.quantize_mx(
+            out=codes[:, t, :].bitcast(FP8X4),
+            scales=scales[:, t, :],
+            in_=grouped[:, t * C : (t + 1) * C],
+        )
     return codes, scales
 
 
@@ -88,71 +96,68 @@ def tile_attgcn_pa_s_kernel(
             out=lam_kappa_b[:], in0=kappa_b_bf[:], scalar1=lam_f[:, 0:1], scalar2=None, op0=ALU.mult
         )
 
+        x_codes = keep.tile([P, T, N_MIN], U32, align_bytes=64)
+        x_scales = keep.tile([P, T, N_MIN], U8, align_bytes=64)
+        nc.vector.memset(x_codes[:].rearrange("q s n -> q (s n)").bitcast(I32), 0)
+        nc.vector.memset(x_scales[:].rearrange("q s n -> q (s n)").bitcast(I32), 0)
         x_words = x_sb[:].bitcast(F32).rearrange("r (q h) -> r h q", h=2)
         x_t = psum.tile([P, 2, ROWS], F32, tag="bank7")
         for h in range(2):
             nc.tensor.transpose(x_t[:, h, :], x_words[:, h, :], ident[:])
-        x_grouped = keep.tile([P, ROWS * PACK], BF16, align_bytes=64)
-        x_dst = x_grouped[:].bitcast(F32).rearrange("q (b v s h) -> q b v s h", b=B, v=V, s=T)
-        x_src = x_t[:].rearrange("q h (b s v) -> q b v s h", b=B, s=T)
+        x_grouped = keep.tile([P, T, POSES * PACK], BF16, align_bytes=64)
+        x_dst = x_grouped[:].rearrange("q s n -> q (s n)").bitcast(F32)
+        x_dst = x_dst.rearrange("q (s b v h) -> q b s v h", s=T, b=B, h=2)
+        x_src = x_t[:].rearrange("q h (b s v) -> q b s v h", b=B, s=T)
         for b in range(B):
             nc.vector.tensor_copy(out=x_dst[:, b], in_=x_src[:, b])
-        x_codes = keep.tile([P, ROWS], U32, align_bytes=64)
-        x_scales = keep.tile([P, ROWS], U8, align_bytes=64)
-        nc.vector.quantize_mx(out=x_codes[:].bitcast(FP8X4), scales=x_scales[:], in_=x_grouped[:])
+        for s in range(T):
+            nc.vector.quantize_mx(
+                out=x_codes[:, s, 0:POSES].bitcast(FP8X4),
+                scales=x_scales[:, s, 0:POSES],
+                in_=x_grouped[:, s, :],
+            )
 
         def project(raw, name, bank):
             grouped = regroup_weight(nc, keep, raw, name, VECTOR_GROUPS)
             codes, scales = quantise_weight(nc, keep, grouped, name)
-            acc = psum.tile([P, PACK, ROWS], F32, tag=bank, name=name + "_acc")
+            acc = psum.tile([P, PACK, N_MIN], F32, tag=bank, name=name + "_acc")
             for t in range(PACK):
-                cols = slice(t * P, (t + 1) * P)
-                nc.tensor.matmul_mx(
-                    out=acc[:, t, :],
-                    lhsT=codes[:, cols].bitcast(FP8X4),
-                    lhsT_scale=scales[:, cols],
-                    rhs=x_codes[:].bitcast(FP8X4),
-                    rhs_scale=x_scales[:],
-                    start=True,
-                    stop=True,
-                )
+                for s in range(T):
+                    nc.tensor.matmul_mx(
+                        out=acc[:, t, :],
+                        lhsT=codes[:, t, :].bitcast(FP8X4),
+                        lhsT_scale=scales[:, t, :],
+                        rhs=x_codes[:, s, :].bitcast(FP8X4),
+                        rhs_scale=x_scales[:, s, :],
+                        start=(s == 0),
+                        stop=(s == T - 1),
+                    )
             return acc
-
-        def sum_over_time(acc, name):
-            total = keep.tile([P, B, V, PACK], F32, name=name + "_sum")
-            nc.vector.tensor_reduce(
-                out=total[:].rearrange("q b v t -> q (b v) t"),
-                in_=acc[:].rearrange("q t (n s) -> q n t s", s=T),
-                axis=mybir.AxisListType.X,
-                op=ALU.add,
-            )
-            return total
 
         phi_acc = project(phi_raw, "phi", "bank5")
         theta_acc = project(theta_raw, "theta", "bank6")
-        kappa_grouped = regroup_weight(nc, keep, kappa_raw, "kappa", 0)
 
-        phi_sum = sum_over_time(phi_acc, "phi")
         phi_biased = keep.tile([P, B, V, PACK], F32)
         nc.vector.scalar_tensor_tensor(
             out=phi_biased[:].rearrange("q b v t -> q (b v) t"),
-            in0=bias_diff[:].unsqueeze(1).to_broadcast([P, B * V, PACK]),
+            in0=bias_diff[:].unsqueeze(1).to_broadcast([P, POSES, PACK]),
             scalar=float(T),
-            in1=phi_sum[:].rearrange("q b v t -> q (b v) t"),
+            in1=phi_acc[:, :, 0:POSES].rearrange("q t n -> q n t"),
             op0=ALU.mult,
             op1=ALU.add,
         )
-        theta_sum = sum_over_time(theta_acc, "theta")
+        kappa_grouped = regroup_weight(nc, keep, kappa_raw, "kappa", KAPPA_VECTOR_GROUPS)
 
         diff = keep.tile([P, B, V, V, PACK], F32)
         f_bf = keep.tile([P, B, V, V, PACK], BF16, align_bytes=64)
         for b in range(B):
+            theta_b_view = theta_acc[:, :, b * V : (b + 1) * V].rearrange("q t v -> q v t")
             for u0 in range(0, V, U_PIECE):
                 us = slice(u0, u0 + U_PIECE)
                 nc.vector.tensor_tensor(
                     out=diff[:, b, us],
                     in0=phi_biased[:, b, us, :].unsqueeze(2).to_broadcast([P, U_PIECE, V, PACK]),
-                    in1=theta_sum[:, b].unsqueeze(1).to_broadcast([P, U_PIECE, V, PACK]),
+                    in1=theta_b_view.unsqueeze(1).to_broadcast([P, U_PIECE, V, PACK]),
                     op=ALU.subtract,
                 )
                 nc.scalar.activation(
@@ -182,12 +187,11 @@ def tile_attgcn_pa_s_kernel(
 
         for b in range(B):
             for m in range(PACK):
-                cols = slice(m * P, (m + 1) * P)
                 g = psum.tile([P, PAIRS], F32, tag="bank%d" % (b * PACK + m), name="g%d%d" % (b, m))
                 nc.tensor.matmul_mx(
                     out=g[:],
-                    lhsT=kappa_codes[:, cols].bitcast(FP8X4),
-                    lhsT_scale=kappa_scales[:, cols],
+                    lhsT=kappa_codes[:, m, :].bitcast(FP8X4),
+                    lhsT_scale=kappa_scales[:, m, :],
                     rhs=f_codes[:, b, :].bitcast(FP8X4),
                     rhs_scale=f_scales[:, b, :],
                     start=True,

@@ -7,7 +7,6 @@ F32 = mybir.dt.float32
 BF16 = mybir.dt.bfloat16
 U32 = mybir.dt.uint32
 U8 = mybir.dt.uint8
-I32 = mybir.dt.int32
 FP8X4 = mybir.dt.float8_e4m3fn_x4
 ALU = mybir.AluOpType
 ACT = mybir.ActivationFunctionType
@@ -16,12 +15,9 @@ P = 128
 PACK = 4
 B, T, V, C = 2, 4, 16, 512
 ROWS = B * T * V
-POSES = B * V
 PAIRS = V * V
-N_MIN = 128
 U_PIECE = 8
 VECTOR_GROUPS = 84
-KAPPA_VECTOR_GROUPS = P - VECTOR_GROUPS
 
 FLOPS = 2 * ROWS * C * C * 2 + 2 * B * PAIRS * C * C
 
@@ -36,18 +32,20 @@ def regroup_weight(nc, pool, raw, name, vector_groups):
     grouped = pool.tile([P, PACK * C], BF16, name=name + "_grouped", align_bytes=64)
     dst = grouped[:].rearrange("p (t q j) -> p q j t", t=PACK, j=PACK)
     src = raw[:].rearrange("p j (q t) -> p q j t", t=PACK)
-    nc.vector.tensor_copy(out=dst[:, 0:vector_groups], in_=src[:, 0:vector_groups])
+    if vector_groups > 0:
+        nc.vector.tensor_copy(out=dst[:, 0:vector_groups], in_=src[:, 0:vector_groups])
     nc.scalar.copy(out=dst[:, vector_groups:P], in_=src[:, vector_groups:P])
     return grouped
 
 
 def quantise_weight(nc, pool, grouped, name):
-    codes = pool.tile([P, PACK, P], U32, name=name + "_codes", align_bytes=64)
-    scales = pool.tile([P, PACK, P], U8, name=name + "_scales", align_bytes=64)
+    codes = pool.tile([P, C], U32, name=name + "_codes", align_bytes=64)
+    scales = pool.tile([P, C], U8, name=name + "_scales", align_bytes=64)
     for t in range(PACK):
+        cols = slice(t * P, (t + 1) * P)
         nc.vector.quantize_mx(
-            out=codes[:, t, :].bitcast(FP8X4),
-            scales=scales[:, t, :],
+            out=codes[:, cols].bitcast(FP8X4),
+            scales=scales[:, cols],
             in_=grouped[:, t * C : (t + 1) * C],
         )
     return codes, scales
@@ -66,18 +64,17 @@ def tile_attgcn_pa_s_kernel(
         nc.sync.dma_start(out=x_sb[:], in_=x.rearrange("b s v f -> (b s v) f"))
         phi_raw = load_weight(nc, keep, phi_w, "phi")
         theta_raw = load_weight(nc, keep, theta_w, "theta")
+        phi_b_bf = keep.tile([P, PACK], BF16)
+        nc.sync.dma_start(out=phi_b_bf[:], in_=phi_b.rearrange("(q t) -> q t", t=PACK))
+        theta_b_bf = keep.tile([P, PACK], BF16)
+        nc.sync.dma_start(out=theta_b_bf[:], in_=theta_b.rearrange("(q t) -> q t", t=PACK))
         kappa_raw = load_weight(nc, keep, kappa_w, "kappa")
         a_bf = keep.tile([P, PACK, PAIRS], BF16)
         nc.sync.dma_start(out=a_bf[:], in_=A.rearrange("(q m) u v -> q m (u v)", m=PACK))
-
-        phi_b_bf = keep.tile([P, PACK], BF16)
-        nc.scalar.dma_start(out=phi_b_bf[:], in_=phi_b.rearrange("(q t) -> q t", t=PACK))
-        theta_b_bf = keep.tile([P, PACK], BF16)
-        nc.scalar.dma_start(out=theta_b_bf[:], in_=theta_b.rearrange("(q t) -> q t", t=PACK))
         kappa_b_bf = keep.tile([P, PACK], BF16)
-        nc.scalar.dma_start(out=kappa_b_bf[:], in_=kappa_b.rearrange("(q m) -> q m", m=PACK))
+        nc.sync.dma_start(out=kappa_b_bf[:], in_=kappa_b.rearrange("(q m) -> q m", m=PACK))
         lam_bf = keep.tile([P, 1], BF16)
-        nc.scalar.dma_start(out=lam_bf[:], in_=lam.partition_broadcast(P))
+        nc.sync.dma_start(out=lam_bf[:], in_=lam.partition_broadcast(P))
 
         warm_in = keep.tile([P, 1], F32)
         nc.vector.memset(warm_in[:], 0.0)
@@ -96,68 +93,71 @@ def tile_attgcn_pa_s_kernel(
             out=lam_kappa_b[:], in0=kappa_b_bf[:], scalar1=lam_f[:, 0:1], scalar2=None, op0=ALU.mult
         )
 
-        x_codes = keep.tile([P, T, N_MIN], U32, align_bytes=64)
-        x_scales = keep.tile([P, T, N_MIN], U8, align_bytes=64)
-        nc.vector.memset(x_codes[:].rearrange("q s n -> q (s n)").bitcast(I32), 0)
-        nc.vector.memset(x_scales[:].rearrange("q s n -> q (s n)").bitcast(I32), 0)
         x_words = x_sb[:].bitcast(F32).rearrange("r (q h) -> r h q", h=2)
         x_t = psum.tile([P, 2, ROWS], F32, tag="bank7")
         for h in range(2):
             nc.tensor.transpose(x_t[:, h, :], x_words[:, h, :], ident[:])
-        x_grouped = keep.tile([P, T, POSES * PACK], BF16, align_bytes=64)
-        x_dst = x_grouped[:].rearrange("q s n -> q (s n)").bitcast(F32)
-        x_dst = x_dst.rearrange("q (s b v h) -> q b s v h", s=T, b=B, h=2)
-        x_src = x_t[:].rearrange("q h (b s v) -> q b s v h", b=B, s=T)
+        x_grouped = keep.tile([P, ROWS * PACK], BF16, align_bytes=64)
+        x_dst = x_grouped[:].bitcast(F32).rearrange("q (b v s h) -> q b v s h", b=B, v=V, s=T)
+        x_src = x_t[:].rearrange("q h (b s v) -> q b v s h", b=B, s=T)
         for b in range(B):
             nc.vector.tensor_copy(out=x_dst[:, b], in_=x_src[:, b])
-        for s in range(T):
-            nc.vector.quantize_mx(
-                out=x_codes[:, s, 0:POSES].bitcast(FP8X4),
-                scales=x_scales[:, s, 0:POSES],
-                in_=x_grouped[:, s, :],
-            )
+        x_codes = keep.tile([P, ROWS], U32, align_bytes=64)
+        x_scales = keep.tile([P, ROWS], U8, align_bytes=64)
+        nc.vector.quantize_mx(out=x_codes[:].bitcast(FP8X4), scales=x_scales[:], in_=x_grouped[:])
 
         def project(raw, name, bank):
             grouped = regroup_weight(nc, keep, raw, name, VECTOR_GROUPS)
             codes, scales = quantise_weight(nc, keep, grouped, name)
-            acc = psum.tile([P, PACK, N_MIN], F32, tag=bank, name=name + "_acc")
+            acc = psum.tile([P, PACK, ROWS], F32, tag=bank, name=name + "_acc")
             for t in range(PACK):
-                for s in range(T):
-                    nc.tensor.matmul_mx(
-                        out=acc[:, t, :],
-                        lhsT=codes[:, t, :].bitcast(FP8X4),
-                        lhsT_scale=scales[:, t, :],
-                        rhs=x_codes[:, s, :].bitcast(FP8X4),
-                        rhs_scale=x_scales[:, s, :],
-                        start=(s == 0),
-                        stop=(s == T - 1),
-                    )
+                cols = slice(t * P, (t + 1) * P)
+                nc.tensor.matmul_mx(
+                    out=acc[:, t, :],
+                    lhsT=codes[:, cols].bitcast(FP8X4),
+                    lhsT_scale=scales[:, cols],
+                    rhs=x_codes[:].bitcast(FP8X4),
+                    rhs_scale=x_scales[:],
+                    start=True,
+                    stop=True,
+                )
             return acc
+
+        def sum_over_time(acc, name):
+            total = keep.tile([P, B, V, PACK], F32, name=name + "_sum")
+            nc.vector.tensor_reduce(
+                out=total[:].rearrange("q b v t -> q (b v) t"),
+                in_=acc[:].rearrange("q t (n s) -> q n t s", s=T),
+                axis=mybir.AxisListType.X,
+                op=ALU.add,
+            )
+            return total
 
         phi_acc = project(phi_raw, "phi", "bank5")
         theta_acc = project(theta_raw, "theta", "bank6")
+        kappa_grouped = regroup_weight(nc, keep, kappa_raw, "kappa", 0)
 
+        phi_sum = sum_over_time(phi_acc, "phi")
         phi_biased = keep.tile([P, B, V, PACK], F32)
         nc.vector.scalar_tensor_tensor(
             out=phi_biased[:].rearrange("q b v t -> q (b v) t"),
-            in0=bias_diff[:].unsqueeze(1).to_broadcast([P, POSES, PACK]),
+            in0=bias_diff[:].unsqueeze(1).to_broadcast([P, B * V, PACK]),
             scalar=float(T),
-            in1=phi_acc[:, :, 0:POSES].rearrange("q t n -> q n t"),
+            in1=phi_sum[:].rearrange("q b v t -> q (b v) t"),
             op0=ALU.mult,
             op1=ALU.add,
         )
-        kappa_grouped = regroup_weight(nc, keep, kappa_raw, "kappa", KAPPA_VECTOR_GROUPS)
+        theta_sum = sum_over_time(theta_acc, "theta")
 
         diff = keep.tile([P, B, V, V, PACK], F32)
         f_bf = keep.tile([P, B, V, V, PACK], BF16, align_bytes=64)
         for b in range(B):
-            theta_b_view = theta_acc[:, :, b * V : (b + 1) * V].rearrange("q t v -> q v t")
             for u0 in range(0, V, U_PIECE):
                 us = slice(u0, u0 + U_PIECE)
                 nc.vector.tensor_tensor(
                     out=diff[:, b, us],
                     in0=phi_biased[:, b, us, :].unsqueeze(2).to_broadcast([P, U_PIECE, V, PACK]),
-                    in1=theta_b_view.unsqueeze(1).to_broadcast([P, U_PIECE, V, PACK]),
+                    in1=theta_sum[:, b].unsqueeze(1).to_broadcast([P, U_PIECE, V, PACK]),
                     op=ALU.subtract,
                 )
                 nc.scalar.activation(
@@ -167,18 +167,21 @@ def tile_attgcn_pa_s_kernel(
                     scale=1.0 / T,
                 )
 
-        kappa_codes, kappa_scales = quantise_weight(nc, keep, kappa_grouped, "kappa")
-
         f_codes = keep.tile([P, B, PAIRS], U32, align_bytes=64)
         f_scales = keep.tile([P, B, PAIRS], U8, align_bytes=64)
         out_sb = keep.tile([P, B, PACK, PAIRS], F32)
         out_view = out.rearrange("b (q m) u v -> b q m (u v)", m=PACK)
-        for b in range(B):
+
+        def quantise_f(b):
             nc.vector.quantize_mx(
                 out=f_codes[:, b, :].bitcast(FP8X4),
                 scales=f_scales[:, b, :],
                 in_=f_bf[:, b].rearrange("q u v t -> q (u v t)"),
             )
+
+        quantise_f(0)
+        kappa_codes, kappa_scales = quantise_weight(nc, keep, kappa_grouped, "kappa")
+        quantise_f(1)
         a_plus = keep.tile([P, PACK, PAIRS], F32)
         for m in range(PACK):
             nc.scalar.activation(
@@ -187,11 +190,12 @@ def tile_attgcn_pa_s_kernel(
 
         for b in range(B):
             for m in range(PACK):
+                cols = slice(m * P, (m + 1) * P)
                 g = psum.tile([P, PAIRS], F32, tag="bank%d" % (b * PACK + m), name="g%d%d" % (b, m))
                 nc.tensor.matmul_mx(
                     out=g[:],
-                    lhsT=kappa_codes[:, m, :].bitcast(FP8X4),
-                    lhsT_scale=kappa_scales[:, m, :],
+                    lhsT=kappa_codes[:, cols].bitcast(FP8X4),
+                    lhsT_scale=kappa_scales[:, cols],
                     rhs=f_codes[:, b, :].bitcast(FP8X4),
                     rhs_scale=f_scales[:, b, :],
                     start=True,

@@ -17,7 +17,8 @@ B, T, V, C = 2, 4, 16, 512
 ROWS = B * T * V
 PAIRS = V * V
 U_PIECE = 8
-VECTOR_GROUPS = 84
+PHI_VECTOR_GROUPS = 84
+THETA_VECTOR_GROUPS = 64
 
 FLOPS = 2 * ROWS * C * C * 2 + 2 * B * PAIRS * C * C
 
@@ -41,14 +42,16 @@ def regroup_weight(nc, pool, raw, name, vector_groups):
 def quantise_weight(nc, pool, grouped, name):
     codes = pool.tile([P, C], U32, name=name + "_codes", align_bytes=64)
     scales = pool.tile([P, C], U8, name=name + "_scales", align_bytes=64)
-    for t in range(PACK):
-        cols = slice(t * P, (t + 1) * P)
+
+    def quantise_tiles(t0, t1):
+        cols = slice(t0 * P, t1 * P)
         nc.vector.quantize_mx(
             out=codes[:, cols].bitcast(FP8X4),
             scales=scales[:, cols],
-            in_=grouped[:, t * C : (t + 1) * C],
+            in_=grouped[:, t0 * C : t1 * C],
         )
-    return codes, scales
+
+    return codes, scales, quantise_tiles
 
 
 def tile_attgcn_pa_s_kernel(
@@ -64,17 +67,17 @@ def tile_attgcn_pa_s_kernel(
         nc.sync.dma_start(out=x_sb[:], in_=x.rearrange("b s v f -> (b s v) f"))
         phi_raw = load_weight(nc, keep, phi_w, "phi")
         theta_raw = load_weight(nc, keep, theta_w, "theta")
+        kappa_b_bf = keep.tile([P, PACK], BF16)
+        nc.sync.dma_start(out=kappa_b_bf[:], in_=kappa_b.rearrange("(q m) -> q m", m=PACK))
+        lam_bf = keep.tile([P, 1], BF16)
+        nc.sync.dma_start(out=lam_bf[:], in_=lam.partition_broadcast(P))
+        a_bf = keep.tile([P, PACK, PAIRS], BF16)
+        nc.sync.dma_start(out=a_bf[:], in_=A.rearrange("(q m) u v -> q m (u v)", m=PACK))
         phi_b_bf = keep.tile([P, PACK], BF16)
         nc.sync.dma_start(out=phi_b_bf[:], in_=phi_b.rearrange("(q t) -> q t", t=PACK))
         theta_b_bf = keep.tile([P, PACK], BF16)
         nc.sync.dma_start(out=theta_b_bf[:], in_=theta_b.rearrange("(q t) -> q t", t=PACK))
         kappa_raw = load_weight(nc, keep, kappa_w, "kappa")
-        a_bf = keep.tile([P, PACK, PAIRS], BF16)
-        nc.sync.dma_start(out=a_bf[:], in_=A.rearrange("(q m) u v -> q m (u v)", m=PACK))
-        kappa_b_bf = keep.tile([P, PACK], BF16)
-        nc.sync.dma_start(out=kappa_b_bf[:], in_=kappa_b.rearrange("(q m) -> q m", m=PACK))
-        lam_bf = keep.tile([P, 1], BF16)
-        nc.sync.dma_start(out=lam_bf[:], in_=lam.partition_broadcast(P))
 
         warm_in = keep.tile([P, 1], F32)
         nc.vector.memset(warm_in[:], 0.0)
@@ -84,13 +87,16 @@ def tile_attgcn_pa_s_kernel(
         ident = keep.tile([P, P], F32)
         make_identity(nc, ident[:])
 
-        bias_diff = keep.tile([P, PACK], F32)
-        nc.gpsimd.tensor_tensor(out=bias_diff[:], in0=phi_b_bf[:], in1=theta_b_bf[:], op=ALU.subtract)
         lam_f = keep.tile([P, 1], F32)
         nc.gpsimd.tensor_copy(out=lam_f[:], in_=lam_bf[:])
         lam_kappa_b = keep.tile([P, PACK], F32)
         nc.gpsimd.tensor_scalar(
             out=lam_kappa_b[:], in0=kappa_b_bf[:], scalar1=lam_f[:, 0:1], scalar2=None, op0=ALU.mult
+        )
+        bias_diff = keep.tile([P, PACK], F32)
+        nc.gpsimd.tensor_tensor(out=bias_diff[:], in0=phi_b_bf[:], in1=theta_b_bf[:], op=ALU.subtract)
+        nc.gpsimd.tensor_scalar(
+            out=bias_diff[:], in0=bias_diff[:], scalar1=float(T), scalar2=None, op0=ALU.mult
         )
 
         x_words = x_sb[:].bitcast(F32).rearrange("r (q h) -> r h q", h=2)
@@ -101,16 +107,22 @@ def tile_attgcn_pa_s_kernel(
         x_dst = x_grouped[:].bitcast(F32).rearrange("q (b v s h) -> q b v s h", b=B, v=V, s=T)
         x_src = x_t[:].rearrange("q h (b s v) -> q b v s h", b=B, s=T)
         for b in range(B):
-            nc.vector.tensor_copy(out=x_dst[:, b], in_=x_src[:, b])
+            nc.scalar.copy(out=x_dst[:, b], in_=x_src[:, b])
+        phi_grouped = regroup_weight(nc, keep, phi_raw, "phi", PHI_VECTOR_GROUPS)
         x_codes = keep.tile([P, ROWS], U32, align_bytes=64)
         x_scales = keep.tile([P, ROWS], U8, align_bytes=64)
         nc.vector.quantize_mx(out=x_codes[:].bitcast(FP8X4), scales=x_scales[:], in_=x_grouped[:])
 
-        def project(raw, name, bank):
-            grouped = regroup_weight(nc, keep, raw, name, VECTOR_GROUPS)
-            codes, scales = quantise_weight(nc, keep, grouped, name)
+        def project(grouped, name, bank):
+            codes, scales, quantise_tiles = quantise_weight(nc, keep, grouped, name)
             acc = psum.tile([P, PACK, ROWS], F32, tag=bank, name=name + "_acc")
-            for t in range(PACK):
+            return acc, codes, scales, quantise_tiles
+
+        def project_half(projection, h):
+            acc, codes, scales, quantise_tiles = projection
+            t0, t1 = h * PACK // 2, (h + 1) * PACK // 2
+            quantise_tiles(t0, t1)
+            for t in range(t0, t1):
                 cols = slice(t * P, (t + 1) * P)
                 nc.tensor.matmul_mx(
                     out=acc[:, t, :],
@@ -121,7 +133,6 @@ def tile_attgcn_pa_s_kernel(
                     start=True,
                     stop=True,
                 )
-            return acc
 
         def sum_over_time(acc, name):
             total = keep.tile([P, B, V, PACK], F32, name=name + "_sum")
@@ -133,44 +144,50 @@ def tile_attgcn_pa_s_kernel(
             )
             return total
 
-        phi_acc = project(phi_raw, "phi", "bank5")
-        theta_acc = project(theta_raw, "theta", "bank6")
+        phi_projection = project(phi_grouped, "phi", "bank5")
+        project_half(phi_projection, 0)
+        theta_grouped = regroup_weight(nc, keep, theta_raw, "theta", THETA_VECTOR_GROUPS)
+        theta_projection = project(theta_grouped, "theta", "bank6")
+        project_half(phi_projection, 1)
+        project_half(theta_projection, 0)
+        project_half(theta_projection, 1)
+
+        a_plus = keep.tile([P, PACK, PAIRS], F32)
+        for m in range(PACK):
+            nc.scalar.activation(
+                out=a_plus[:, m, :], in_=a_bf[:, m, :], func=ACT.Identity, bias=lam_kappa_b[:, m : m + 1]
+            )
         kappa_grouped = regroup_weight(nc, keep, kappa_raw, "kappa", 0)
 
-        phi_sum = sum_over_time(phi_acc, "phi")
+        phi_sum = sum_over_time(phi_projection[0], "phi")
         phi_biased = keep.tile([P, B, V, PACK], F32)
-        nc.vector.scalar_tensor_tensor(
+        nc.gpsimd.tensor_tensor(
             out=phi_biased[:].rearrange("q b v t -> q (b v) t"),
-            in0=bias_diff[:].unsqueeze(1).to_broadcast([P, B * V, PACK]),
-            scalar=float(T),
-            in1=phi_sum[:].rearrange("q b v t -> q (b v) t"),
-            op0=ALU.mult,
-            op1=ALU.add,
+            in0=phi_sum[:].rearrange("q b v t -> q (b v) t"),
+            in1=bias_diff[:].unsqueeze(1).to_broadcast([P, B * V, PACK]),
+            op=ALU.add,
         )
-        theta_sum = sum_over_time(theta_acc, "theta")
+        theta_sum = sum_over_time(theta_projection[0], "theta")
 
         diff = keep.tile([P, B, V, V, PACK], F32)
         f_bf = keep.tile([P, B, V, V, PACK], BF16, align_bytes=64)
-        for b in range(B):
-            for u0 in range(0, V, U_PIECE):
-                us = slice(u0, u0 + U_PIECE)
-                nc.vector.tensor_tensor(
-                    out=diff[:, b, us],
-                    in0=phi_biased[:, b, us, :].unsqueeze(2).to_broadcast([P, U_PIECE, V, PACK]),
-                    in1=theta_sum[:, b].unsqueeze(1).to_broadcast([P, U_PIECE, V, PACK]),
-                    op=ALU.subtract,
-                )
-                nc.scalar.activation(
-                    out=f_bf[:, b, us].rearrange("q u v t -> q (u v t)"),
-                    in_=diff[:, b, us].rearrange("q u v t -> q (u v t)"),
-                    func=ACT.Tanh,
-                    scale=1.0 / T,
-                )
-
         f_codes = keep.tile([P, B, PAIRS], U32, align_bytes=64)
         f_scales = keep.tile([P, B, PAIRS], U8, align_bytes=64)
-        out_sb = keep.tile([P, B, PACK, PAIRS], F32)
-        out_view = out.rearrange("b (q m) u v -> b q m (u v)", m=PACK)
+
+        def difference_and_tanh(b, u0):
+            us = slice(u0, u0 + U_PIECE)
+            nc.vector.tensor_tensor(
+                out=diff[:, b, us],
+                in0=phi_biased[:, b, us, :].unsqueeze(2).to_broadcast([P, U_PIECE, V, PACK]),
+                in1=theta_sum[:, b].unsqueeze(1).to_broadcast([P, U_PIECE, V, PACK]),
+                op=ALU.subtract,
+            )
+            nc.scalar.activation(
+                out=f_bf[:, b, us].rearrange("q u v t -> q (u v t)"),
+                in_=diff[:, b, us].rearrange("q u v t -> q (u v t)"),
+                func=ACT.Tanh,
+                scale=1.0 / T,
+            )
 
         def quantise_f(b):
             nc.vector.quantize_mx(
@@ -179,34 +196,38 @@ def tile_attgcn_pa_s_kernel(
                 in_=f_bf[:, b].rearrange("q u v t -> q (u v t)"),
             )
 
-        quantise_f(0)
-        kappa_codes, kappa_scales = quantise_weight(nc, keep, kappa_grouped, "kappa")
-        quantise_f(1)
-        a_plus = keep.tile([P, PACK, PAIRS], F32)
-        for m in range(PACK):
-            nc.scalar.activation(
-                out=a_plus[:, m, :], in_=a_bf[:, m, :], func=ACT.Identity, bias=lam_kappa_b[:, m : m + 1]
+        out_sb = keep.tile([P, B, PACK, PAIRS], F32)
+        out_view = out.rearrange("b (q m) u v -> b q m (u v)", m=PACK)
+
+        def finish(b, m):
+            cols = slice(m * P, (m + 1) * P)
+            g = psum.tile([P, PAIRS], F32, tag="bank%d" % (b * PACK + m), name="g%d%d" % (b, m))
+            nc.tensor.matmul_mx(
+                out=g[:],
+                lhsT=kappa_codes[:, cols].bitcast(FP8X4),
+                lhsT_scale=kappa_scales[:, cols],
+                rhs=f_codes[:, b, :].bitcast(FP8X4),
+                rhs_scale=f_scales[:, b, :],
+                start=True,
+                stop=True,
             )
+            nc.vector.scalar_tensor_tensor(
+                out=out_sb[:, b, m, :],
+                in0=g[:],
+                scalar=lam_f[:, 0:1],
+                in1=a_plus[:, m, :],
+                op0=ALU.mult,
+                op1=ALU.add,
+            )
+            nc.sync.dma_start(out=out_view[b, :, m, :], in_=out_sb[:, b, m, :])
 
         for b in range(B):
+            for u0 in range(0, V, U_PIECE):
+                difference_and_tanh(b, u0)
+        kappa_codes, kappa_scales, quantise_kappa = quantise_weight(nc, keep, kappa_grouped, "kappa")
+        quantise_kappa(0, PACK)
+        for b in range(B):
+            quantise_f(b)
+        for b in range(B):
             for m in range(PACK):
-                cols = slice(m * P, (m + 1) * P)
-                g = psum.tile([P, PAIRS], F32, tag="bank%d" % (b * PACK + m), name="g%d%d" % (b, m))
-                nc.tensor.matmul_mx(
-                    out=g[:],
-                    lhsT=kappa_codes[:, cols].bitcast(FP8X4),
-                    lhsT_scale=kappa_scales[:, cols],
-                    rhs=f_codes[:, b, :].bitcast(FP8X4),
-                    rhs_scale=f_scales[:, b, :],
-                    start=True,
-                    stop=True,
-                )
-                nc.vector.scalar_tensor_tensor(
-                    out=out_sb[:, b, m, :],
-                    in0=g[:],
-                    scalar=lam_f[:, 0:1],
-                    in1=a_plus[:, m, :],
-                    op0=ALU.mult,
-                    op1=ALU.add,
-                )
-                nc.sync.dma_start(out=out_view[b, :, m, :], in_=out_sb[:, b, m, :])
+                finish(b, m)

@@ -67,17 +67,17 @@ def tile_attgcn_pa_s_kernel(
         nc.sync.dma_start(out=x_sb[:], in_=x.rearrange("b s v f -> (b s v) f"))
         phi_raw = load_weight(nc, keep, phi_w, "phi")
         theta_raw = load_weight(nc, keep, theta_w, "theta")
-        kappa_b_bf = keep.tile([P, PACK], BF16)
-        nc.sync.dma_start(out=kappa_b_bf[:], in_=kappa_b.rearrange("(q m) -> q m", m=PACK))
-        lam_bf = keep.tile([P, 1], BF16)
-        nc.sync.dma_start(out=lam_bf[:], in_=lam.partition_broadcast(P))
-        a_bf = keep.tile([P, PACK, PAIRS], BF16)
-        nc.sync.dma_start(out=a_bf[:], in_=A.rearrange("(q m) u v -> q m (u v)", m=PACK))
         phi_b_bf = keep.tile([P, PACK], BF16)
         nc.sync.dma_start(out=phi_b_bf[:], in_=phi_b.rearrange("(q t) -> q t", t=PACK))
         theta_b_bf = keep.tile([P, PACK], BF16)
         nc.sync.dma_start(out=theta_b_bf[:], in_=theta_b.rearrange("(q t) -> q t", t=PACK))
         kappa_raw = load_weight(nc, keep, kappa_w, "kappa")
+        a_bf = keep.tile([P, PACK, PAIRS], BF16)
+        nc.sync.dma_start(out=a_bf[:], in_=A.rearrange("(q m) u v -> q m (u v)", m=PACK))
+        kappa_b_bf = keep.tile([P, PACK], BF16)
+        nc.sync.dma_start(out=kappa_b_bf[:], in_=kappa_b.rearrange("(q m) -> q m", m=PACK))
+        lam_bf = keep.tile([P, 1], BF16)
+        nc.sync.dma_start(out=lam_bf[:], in_=lam.partition_broadcast(P))
 
         warm_in = keep.tile([P, 1], F32)
         nc.vector.memset(warm_in[:], 0.0)
@@ -87,16 +87,16 @@ def tile_attgcn_pa_s_kernel(
         ident = keep.tile([P, P], F32)
         make_identity(nc, ident[:])
 
+        bias_diff = keep.tile([P, PACK], F32)
+        nc.gpsimd.tensor_tensor(out=bias_diff[:], in0=phi_b_bf[:], in1=theta_b_bf[:], op=ALU.subtract)
+        nc.gpsimd.tensor_scalar(
+            out=bias_diff[:], in0=bias_diff[:], scalar1=float(T), scalar2=None, op0=ALU.mult
+        )
         lam_f = keep.tile([P, 1], F32)
         nc.gpsimd.tensor_copy(out=lam_f[:], in_=lam_bf[:])
         lam_kappa_b = keep.tile([P, PACK], F32)
         nc.gpsimd.tensor_scalar(
             out=lam_kappa_b[:], in0=kappa_b_bf[:], scalar1=lam_f[:, 0:1], scalar2=None, op0=ALU.mult
-        )
-        bias_diff = keep.tile([P, PACK], F32)
-        nc.gpsimd.tensor_tensor(out=bias_diff[:], in0=phi_b_bf[:], in1=theta_b_bf[:], op=ALU.subtract)
-        nc.gpsimd.tensor_scalar(
-            out=bias_diff[:], in0=bias_diff[:], scalar1=float(T), scalar2=None, op0=ALU.mult
         )
 
         x_words = x_sb[:].bitcast(F32).rearrange("r (q h) -> r h q", h=2)
@@ -152,11 +152,6 @@ def tile_attgcn_pa_s_kernel(
         project_half(theta_projection, 0)
         project_half(theta_projection, 1)
 
-        a_plus = keep.tile([P, PACK, PAIRS], F32)
-        for m in range(PACK):
-            nc.scalar.activation(
-                out=a_plus[:, m, :], in_=a_bf[:, m, :], func=ACT.Identity, bias=lam_kappa_b[:, m : m + 1]
-            )
         kappa_grouped = regroup_weight(nc, keep, kappa_raw, "kappa", 0)
 
         phi_sum = sum_over_time(phi_projection[0], "phi")
@@ -224,6 +219,11 @@ def tile_attgcn_pa_s_kernel(
         for b in range(B):
             for u0 in range(0, V, U_PIECE):
                 difference_and_tanh(b, u0)
+        a_plus = keep.tile([P, PACK, PAIRS], F32)
+        for m in range(PACK):
+            nc.scalar.activation(
+                out=a_plus[:, m, :], in_=a_bf[:, m, :], func=ACT.Identity, bias=lam_kappa_b[:, m : m + 1]
+            )
         kappa_codes, kappa_scales, quantise_kappa = quantise_weight(nc, keep, kappa_grouped, "kappa")
         quantise_kappa(0, PACK)
         for b in range(B):

@@ -20,6 +20,8 @@ U_PIECE = 8
 PHI_VECTOR_GROUPS = 84
 THETA_VECTOR_GROUPS = 64
 
+IDLE_PASSES = 14
+
 FLOPS = 2 * ROWS * C * C * 2 + 2 * B * PAIRS * C * C
 
 
@@ -79,6 +81,11 @@ def tile_attgcn_pa_s_kernel(
         lam_bf = keep.tile([P, 1], BF16)
         nc.sync.dma_start(out=lam_bf[:], in_=lam.partition_broadcast(P))
 
+        x_codes = keep.tile([P, ROWS + ROWS // 2], U32, align_bytes=64)
+        x_scales = keep.tile([P, ROWS + ROWS // 2], U8, align_bytes=64)
+        nc.vector.memset(x_codes[:, ROWS:], 0)
+        nc.vector.memset(x_scales[:, ROWS:], 0)
+
         warm_in = keep.tile([P, 1], F32)
         nc.vector.memset(warm_in[:], 0.0)
         warm_out = keep.tile([P, 1], F32)
@@ -86,6 +93,14 @@ def tile_attgcn_pa_s_kernel(
 
         ident = keep.tile([P, P], F32)
         make_identity(nc, ident[:])
+
+        early = psum.tile([P, P], F32, tag="bank0", name="early")
+
+        def warm(passes):
+            for i in range(passes):
+                nc.tensor.matmul(early[:], lhsT=ident[:], rhs=ident[:], start=True, stop=True)
+
+        warm(2)
 
         bias_diff = keep.tile([P, PACK], F32)
         nc.gpsimd.tensor_tensor(out=bias_diff[:], in0=phi_b_bf[:], in1=theta_b_bf[:], op=ALU.subtract)
@@ -103,15 +118,16 @@ def tile_attgcn_pa_s_kernel(
         x_t = psum.tile([P, 2, ROWS], F32, tag="bank7")
         for h in range(2):
             nc.tensor.transpose(x_t[:, h, :], x_words[:, h, :], ident[:])
+        warm(3)
         x_grouped = keep.tile([P, ROWS * PACK], BF16, align_bytes=64)
-        x_dst = x_grouped[:].bitcast(F32).rearrange("q (b v s h) -> q b v s h", b=B, v=V, s=T)
-        x_src = x_t[:].rearrange("q h (b s v) -> q b v s h", b=B, s=T)
+        x_dst = x_grouped[:].bitcast(F32).rearrange("q (s b v h) -> q b s v h", b=B, v=V, s=T)
+        x_src = x_t[:].rearrange("q h (b s v) -> q b s v h", b=B, s=T)
         for b in range(B):
             nc.scalar.copy(out=x_dst[:, b], in_=x_src[:, b])
         phi_grouped = regroup_weight(nc, keep, phi_raw, "phi", PHI_VECTOR_GROUPS)
-        x_codes = keep.tile([P, ROWS], U32, align_bytes=64)
-        x_scales = keep.tile([P, ROWS], U8, align_bytes=64)
-        nc.vector.quantize_mx(out=x_codes[:].bitcast(FP8X4), scales=x_scales[:], in_=x_grouped[:])
+        nc.vector.quantize_mx(
+            out=x_codes[:, 0:ROWS].bitcast(FP8X4), scales=x_scales[:, 0:ROWS], in_=x_grouped[:]
+        )
 
         def project(grouped, name, bank):
             codes, scales, quantise_tiles = quantise_weight(nc, keep, grouped, name)
@@ -124,21 +140,23 @@ def tile_attgcn_pa_s_kernel(
             quantise_tiles(t0, t1)
             for t in range(t0, t1):
                 cols = slice(t * P, (t + 1) * P)
-                nc.tensor.matmul_mx(
-                    out=acc[:, t, :],
-                    lhsT=codes[:, cols].bitcast(FP8X4),
-                    lhsT_scale=scales[:, cols],
-                    rhs=x_codes[:].bitcast(FP8X4),
-                    rhs_scale=x_scales[:],
-                    start=True,
-                    stop=True,
-                )
+                for first in (0, ROWS // 2):
+                    rows = slice(first, first + ROWS)
+                    nc.tensor.matmul_mx(
+                        out=acc[:, t, :],
+                        lhsT=codes[:, cols].bitcast(FP8X4),
+                        lhsT_scale=scales[:, cols],
+                        rhs=x_codes[:, rows].bitcast(FP8X4),
+                        rhs_scale=x_scales[:, rows],
+                        start=first == 0,
+                        stop=first > 0,
+                    )
 
         def sum_over_time(acc, name):
             total = keep.tile([P, B, V, PACK], F32, name=name + "_sum")
             nc.vector.tensor_reduce(
                 out=total[:].rearrange("q b v t -> q (b v) t"),
-                in_=acc[:].rearrange("q t (n s) -> q n t s", s=T),
+                in_=acc[:, :, 0 : ROWS // 2].rearrange("q t (s n) -> q n t s", s=T // 2),
                 axis=mybir.AxisListType.X,
                 op=ALU.add,
             )
@@ -219,6 +237,18 @@ def tile_attgcn_pa_s_kernel(
         for b in range(B):
             for u0 in range(0, V, U_PIECE):
                 difference_and_tanh(b, u0)
+        idle = psum.tile([P, C], F32, tag="bank0", name="idle")
+        for i in range(IDLE_PASSES):
+            nc.tensor.matmul_mx(
+                out=idle[:],
+                lhsT=phi_projection[1][:, 0:P].bitcast(FP8X4),
+                lhsT_scale=phi_projection[2][:, 0:P],
+                rhs=theta_projection[1][:].bitcast(FP8X4),
+                rhs_scale=theta_projection[2][:],
+                start=True,
+                stop=True,
+            )
+
         a_plus = keep.tile([P, PACK, PAIRS], F32)
         for m in range(PACK):
             nc.scalar.activation(

@@ -20,7 +20,7 @@ U_PIECE = 8
 PHI_VECTOR_GROUPS = 84
 THETA_VECTOR_GROUPS = 64
 
-IDLE_PASSES = 14
+IDLE_PASSES = 11
 
 FLOPS = 2 * ROWS * C * C * 2 + 2 * B * PAIRS * C * C
 
@@ -118,7 +118,7 @@ def tile_attgcn_pa_s_kernel(
         x_t = psum.tile([P, 2, ROWS], F32, tag="bank7")
         for h in range(2):
             nc.tensor.transpose(x_t[:, h, :], x_words[:, h, :], ident[:])
-        warm(3)
+        warm(6)
         x_grouped = keep.tile([P, ROWS * PACK], BF16, align_bytes=64)
         x_dst = x_grouped[:].bitcast(F32).rearrange("q (s b v h) -> q b s v h", b=B, v=V, s=T)
         x_src = x_t[:].rearrange("q h (b s v) -> q b s v h", b=B, s=T)

@@ -16,7 +16,6 @@ PACK = 4
 B, T, V, C = 2, 4, 16, 512
 ROWS = B * T * V
 PAIRS = V * V
-U_PIECE = 8
 PHI_VECTOR_GROUPS = 84
 THETA_VECTOR_GROUPS = 64
 
@@ -74,12 +73,12 @@ def tile_attgcn_pa_s_kernel(
         theta_b_bf = keep.tile([P, PACK], BF16)
         nc.sync.dma_start(out=theta_b_bf[:], in_=theta_b.rearrange("(q t) -> q t", t=PACK))
         kappa_raw = load_weight(nc, keep, kappa_w, "kappa")
-        a_bf = keep.tile([P, PACK, PAIRS], BF16)
-        nc.sync.dma_start(out=a_bf[:], in_=A.rearrange("(q m) u v -> q m (u v)", m=PACK))
         kappa_b_bf = keep.tile([P, PACK], BF16)
         nc.sync.dma_start(out=kappa_b_bf[:], in_=kappa_b.rearrange("(q m) -> q m", m=PACK))
         lam_bf = keep.tile([P, 1], BF16)
         nc.sync.dma_start(out=lam_bf[:], in_=lam.partition_broadcast(P))
+        a_bf = keep.tile([P, PACK, PAIRS], BF16)
+        nc.sync.dma_start(out=a_bf[:], in_=A.rearrange("(q m) u v -> q m (u v)", m=PACK))
 
         x_codes = keep.tile([P, ROWS + ROWS // 2], U32, align_bytes=64)
         x_scales = keep.tile([P, ROWS + ROWS // 2], U8, align_bytes=64)
@@ -104,9 +103,6 @@ def tile_attgcn_pa_s_kernel(
 
         bias_diff = keep.tile([P, PACK], F32)
         nc.gpsimd.tensor_tensor(out=bias_diff[:], in0=phi_b_bf[:], in1=theta_b_bf[:], op=ALU.subtract)
-        nc.gpsimd.tensor_scalar(
-            out=bias_diff[:], in0=bias_diff[:], scalar1=float(T), scalar2=None, op0=ALU.mult
-        )
         lam_f = keep.tile([P, 1], F32)
         nc.gpsimd.tensor_copy(out=lam_f[:], in_=lam_bf[:])
         lam_kappa_b = keep.tile([P, PACK], F32)
@@ -152,15 +148,14 @@ def tile_attgcn_pa_s_kernel(
                         stop=first > 0,
                     )
 
-        def sum_over_time(acc, name):
-            total = keep.tile([P, B, V, PACK], F32, name=name + "_sum")
+        def sum_over_time(total, acc, b0, b1):
+            n0, n1 = b0 * V, b1 * V
             nc.vector.tensor_reduce(
-                out=total[:].rearrange("q b v t -> q (b v) t"),
-                in_=acc[:, :, 0 : ROWS // 2].rearrange("q t (s n) -> q n t s", s=T // 2),
+                out=total[:, n0:n1],
+                in_=acc[:, :, 0 : ROWS // 2].rearrange("q t (s n) -> q n t s", s=T // 2)[:, n0:n1],
                 axis=mybir.AxisListType.X,
                 op=ALU.add,
             )
-            return total
 
         phi_projection = project(phi_grouped, "phi", "bank5")
         project_half(phi_projection, 0)
@@ -172,27 +167,32 @@ def tile_attgcn_pa_s_kernel(
 
         kappa_grouped = regroup_weight(nc, keep, kappa_raw, "kappa", 0)
 
-        phi_sum = sum_over_time(phi_projection[0], "phi")
-        phi_biased = keep.tile([P, B, V, PACK], F32)
-        nc.gpsimd.tensor_tensor(
-            out=phi_biased[:].rearrange("q b v t -> q (b v) t"),
-            in0=phi_sum[:].rearrange("q b v t -> q (b v) t"),
-            in1=bias_diff[:].unsqueeze(1).to_broadcast([P, B * V, PACK]),
-            op=ALU.add,
+        phi_sum = keep.tile([P, B * V, PACK], F32)
+        sum_over_time(phi_sum, phi_projection[0], 0, B)
+        phi_biased = keep.tile([P, B * V, PACK], F32)
+        nc.vector.scalar_tensor_tensor(
+            out=phi_biased[:],
+            in0=bias_diff[:].unsqueeze(1).to_broadcast([P, B * V, PACK]),
+            scalar=float(T),
+            in1=phi_sum[:],
+            op0=ALU.mult,
+            op1=ALU.add,
         )
-        theta_sum = sum_over_time(theta_projection[0], "theta")
+        theta_sum = keep.tile([P, B * V, PACK], F32)
+        for b in range(B):
+            sum_over_time(theta_sum, theta_projection[0], b, b + 1)
 
         diff = keep.tile([P, B, V, V, PACK], F32)
         f_bf = keep.tile([P, B, V, V, PACK], BF16, align_bytes=64)
         f_codes = keep.tile([P, B, PAIRS], U32, align_bytes=64)
         f_scales = keep.tile([P, B, PAIRS], U8, align_bytes=64)
 
-        def difference_and_tanh(b, u0):
-            us = slice(u0, u0 + U_PIECE)
+        def difference_and_tanh(b, u0, u1):
+            us = slice(u0, u1)
             nc.vector.tensor_tensor(
                 out=diff[:, b, us],
-                in0=phi_biased[:, b, us, :].unsqueeze(2).to_broadcast([P, U_PIECE, V, PACK]),
-                in1=theta_sum[:, b].unsqueeze(1).to_broadcast([P, U_PIECE, V, PACK]),
+                in0=phi_biased[:, b * V + u0 : b * V + u1].unsqueeze(2).to_broadcast([P, u1 - u0, V, PACK]),
+                in1=theta_sum[:, b * V : (b + 1) * V].unsqueeze(1).to_broadcast([P, u1 - u0, V, PACK]),
                 op=ALU.subtract,
             )
             nc.scalar.activation(
@@ -202,11 +202,12 @@ def tile_attgcn_pa_s_kernel(
                 scale=1.0 / T,
             )
 
-        def quantise_f(b):
+        def quantise_f(b, u0, u1):
+            pairs = slice(u0 * V, u1 * V)
             nc.vector.quantize_mx(
-                out=f_codes[:, b, :].bitcast(FP8X4),
-                scales=f_scales[:, b, :],
-                in_=f_bf[:, b].rearrange("q u v t -> q (u v t)"),
+                out=f_codes[:, b, pairs].bitcast(FP8X4),
+                scales=f_scales[:, b, pairs],
+                in_=f_bf[:, b, u0:u1].rearrange("q u v t -> q (u v t)"),
             )
 
         out_sb = keep.tile([P, B, PACK, PAIRS], F32)
@@ -234,9 +235,6 @@ def tile_attgcn_pa_s_kernel(
             )
             nc.sync.dma_start(out=out_view[b, :, m, :], in_=out_sb[:, b, m, :])
 
-        for b in range(B):
-            for u0 in range(0, V, U_PIECE):
-                difference_and_tanh(b, u0)
         idle = psum.tile([P, C], F32, tag="bank0", name="idle")
         for i in range(IDLE_PASSES):
             nc.tensor.matmul_mx(
@@ -250,14 +248,29 @@ def tile_attgcn_pa_s_kernel(
             )
 
         a_plus = keep.tile([P, PACK, PAIRS], F32)
-        for m in range(PACK):
+
+        def add_bias_to_a(m):
             nc.scalar.activation(
                 out=a_plus[:, m, :], in_=a_bf[:, m, :], func=ACT.Identity, bias=lam_kappa_b[:, m : m + 1]
             )
+
         kappa_codes, kappa_scales, quantise_kappa = quantise_weight(nc, keep, kappa_grouped, "kappa")
+        add_bias_to_a(0)
+        add_bias_to_a(1)
+        difference_and_tanh(0, 0, 8)
+        difference_and_tanh(0, 8, 16)
+        difference_and_tanh(1, 0, 8)
         quantise_kappa(0, PACK)
-        for b in range(B):
-            quantise_f(b)
-        for b in range(B):
-            for m in range(PACK):
-                finish(b, m)
+        quantise_f(0, 0, V)
+        add_bias_to_a(2)
+        difference_and_tanh(1, 8, 12)
+        difference_and_tanh(1, 12, 16)
+        add_bias_to_a(3)
+        quantise_f(1, 0, 8)
+        finish(0, 0)
+        finish(0, 1)
+        quantise_f(1, 8, 16)
+        finish(0, 2)
+        finish(0, 3)
+        for m in range(PACK):
+            finish(1, m)

@@ -16,43 +16,14 @@ PACK = 4
 B, T, V, C = 2, 4, 16, 512
 ROWS = B * T * V
 PAIRS = V * V
-PHI_VECTOR_GROUPS = 84
-THETA_VECTOR_GROUPS = 64
+STEP = 64
 
-IDLE_PASSES = 11
+PHI_VECTOR = 320
+THETA_VECTOR = 256
+KAPPA_VECTOR = 192
+IDLE_PASSES = 9
 
 FLOPS = 2 * ROWS * C * C * 2 + 2 * B * PAIRS * C * C
-
-
-def load_weight(nc, pool, w, name):
-    raw = pool.tile([P, PACK, C], BF16, name=name + "_raw")
-    nc.sync.dma_start(out=raw[:], in_=w.rearrange("(p j) c -> p j c", j=PACK))
-    return raw
-
-
-def regroup_weight(nc, pool, raw, name, vector_groups):
-    grouped = pool.tile([P, PACK * C], BF16, name=name + "_grouped", align_bytes=64)
-    dst = grouped[:].rearrange("p (t q j) -> p q j t", t=PACK, j=PACK)
-    src = raw[:].rearrange("p j (q t) -> p q j t", t=PACK)
-    if vector_groups > 0:
-        nc.vector.tensor_copy(out=dst[:, 0:vector_groups], in_=src[:, 0:vector_groups])
-    nc.scalar.copy(out=dst[:, vector_groups:P], in_=src[:, vector_groups:P])
-    return grouped
-
-
-def quantise_weight(nc, pool, grouped, name):
-    codes = pool.tile([P, C], U32, name=name + "_codes", align_bytes=64)
-    scales = pool.tile([P, C], U8, name=name + "_scales", align_bytes=64)
-
-    def quantise_tiles(t0, t1):
-        cols = slice(t0 * P, t1 * P)
-        nc.vector.quantize_mx(
-            out=codes[:, cols].bitcast(FP8X4),
-            scales=scales[:, cols],
-            in_=grouped[:, t0 * C : t1 * C],
-        )
-
-    return codes, scales, quantise_tiles
 
 
 def tile_attgcn_pa_s_kernel(
@@ -64,34 +35,40 @@ def tile_attgcn_pa_s_kernel(
         psum = ctx.enter_context(tc.psum_pool(name="psum", bufs=1))
         ctx.enter_context(tc.manual_schedule())
 
-        x_sb = keep.tile([P, C], BF16)
+        vec_rows = keep.tile([P, P], BF16, name="vec_rows")
+        nc.vector.memset(vec_rows[:].bitcast(F32), 0.0)
+        x_sb = keep.tile([P, C], BF16, name="x_sb")
         nc.sync.dma_start(out=x_sb[:], in_=x.rearrange("b s v f -> (b s v) f"))
-        phi_raw = load_weight(nc, keep, phi_w, "phi")
-        theta_raw = load_weight(nc, keep, theta_w, "theta")
-        phi_b_bf = keep.tile([P, PACK], BF16)
-        nc.sync.dma_start(out=phi_b_bf[:], in_=phi_b.rearrange("(q t) -> q t", t=PACK))
-        theta_b_bf = keep.tile([P, PACK], BF16)
-        nc.sync.dma_start(out=theta_b_bf[:], in_=theta_b.rearrange("(q t) -> q t", t=PACK))
-        kappa_raw = load_weight(nc, keep, kappa_w, "kappa")
-        kappa_b_bf = keep.tile([P, PACK], BF16)
-        nc.sync.dma_start(out=kappa_b_bf[:], in_=kappa_b.rearrange("(q m) -> q m", m=PACK))
-        lam_bf = keep.tile([P, 1], BF16)
+        phi_raw = keep.tile([P, PACK, C], BF16, name="phi_raw")
+        nc.sync.dma_start(out=phi_raw[:], in_=phi_w.rearrange("(p j) c -> p j c", j=PACK))
+        theta_raw = keep.tile([P, PACK, C], BF16, name="theta_raw")
+        nc.sync.dma_start(out=theta_raw[:], in_=theta_w.rearrange("(p j) c -> p j c", j=PACK))
+        for i, vec in enumerate((phi_b, theta_b, kappa_b)):
+            nc.sync.dma_start(out=vec_rows[PACK * i : PACK * (i + 1), :], in_=vec.rearrange("(t q) -> t q", t=PACK))
+        kappa_raw = keep.tile([P, PACK, C], BF16, name="kappa_raw")
+        nc.sync.dma_start(out=kappa_raw[:], in_=kappa_w.rearrange("(j p) c -> p j c", j=PACK))
+        lam_bf = keep.tile([P, 1], BF16, name="lam_bf")
         nc.sync.dma_start(out=lam_bf[:], in_=lam.partition_broadcast(P))
-        a_bf = keep.tile([P, PACK, PAIRS], BF16)
-        nc.sync.dma_start(out=a_bf[:], in_=A.rearrange("(q m) u v -> q m (u v)", m=PACK))
+        a_bf = keep.tile([P, PACK, PAIRS], BF16, name="a_bf")
+        nc.sync.dma_start(out=a_bf[:], in_=A.rearrange("(m q) u v -> q m (u v)", m=PACK))
 
-        x_codes = keep.tile([P, ROWS + ROWS // 2], U32, align_bytes=64)
-        x_scales = keep.tile([P, ROWS + ROWS // 2], U8, align_bytes=64)
-        nc.vector.memset(x_codes[:, ROWS:], 0)
-        nc.vector.memset(x_scales[:, ROWS:], 0)
-
-        warm_in = keep.tile([P, 1], F32)
+        x_codes = keep.tile([P, (T + 1) * STEP], U32, name="x_codes", align_bytes=64)
+        x_scales = keep.tile([P, (T + 1) * STEP], U8, name="x_scales", align_bytes=64)
+        nc.vector.memset(x_codes[:, T * STEP :], 0)
+        nc.vector.memset(x_scales[:, T * STEP :], 0)
+        x_grouped = keep.tile([P, T * STEP * PACK], BF16, name="x_grouped", align_bytes=64)
+        nc.vector.memset(
+            x_grouped[:].bitcast(F32).rearrange("q (s n) -> q s n", s=T)[:, :, B * V * PACK // 2 :], 0.0
+        )
+        warm_in = keep.tile([P, 1], F32, name="warm_in")
         nc.vector.memset(warm_in[:], 0.0)
-        warm_out = keep.tile([P, 1], F32)
+        warm_out = keep.tile([P, 1], F32, name="warm_out")
         nc.scalar.activation(out=warm_out[:], in_=warm_in[:], func=ACT.Tanh)
 
-        ident = keep.tile([P, P], F32)
+        ident = keep.tile([P, P], F32, name="ident")
         make_identity(nc, ident[:])
+        ident_bf = keep.tile([P, P], BF16, name="ident_bf")
+        nc.vector.tensor_copy(out=ident_bf[:], in_=ident[:])
 
         early = psum.tile([P, P], F32, tag="bank0", name="early")
 
@@ -101,93 +78,120 @@ def tile_attgcn_pa_s_kernel(
 
         warm(2)
 
-        bias_diff = keep.tile([P, PACK], F32)
-        nc.gpsimd.tensor_tensor(out=bias_diff[:], in0=phi_b_bf[:], in1=theta_b_bf[:], op=ALU.subtract)
-        lam_f = keep.tile([P, 1], F32)
-        nc.gpsimd.tensor_copy(out=lam_f[:], in_=lam_bf[:])
-        lam_kappa_b = keep.tile([P, PACK], F32)
-        nc.gpsimd.tensor_scalar(
-            out=lam_kappa_b[:], in0=kappa_b_bf[:], scalar1=lam_f[:, 0:1], scalar2=None, op0=ALU.mult
-        )
-
         x_words = x_sb[:].bitcast(F32).rearrange("r (q h) -> r h q", h=2)
-        x_t = psum.tile([P, 2, ROWS], F32, tag="bank7")
+        x_t = psum.tile([P, 2, ROWS], F32, tag="bank7", name="x_t")
         for h in range(2):
             nc.tensor.transpose(x_t[:, h, :], x_words[:, h, :], ident[:])
         warm(6)
-        x_grouped = keep.tile([P, ROWS * PACK], BF16, align_bytes=64)
-        x_dst = x_grouped[:].bitcast(F32).rearrange("q (s b v h) -> q b s v h", b=B, v=V, s=T)
+        x_dst = x_grouped[:].bitcast(F32).rearrange("q (s b v h) -> q b s v h", b=STEP // V, v=V, s=T)
         x_src = x_t[:].rearrange("q h (b s v) -> q b s v h", b=B, s=T)
         for b in range(B):
             nc.scalar.copy(out=x_dst[:, b], in_=x_src[:, b])
-        phi_grouped = regroup_weight(nc, keep, phi_raw, "phi", PHI_VECTOR_GROUPS)
-        nc.vector.quantize_mx(
-            out=x_codes[:, 0:ROWS].bitcast(FP8X4), scales=x_scales[:, 0:ROWS], in_=x_grouped[:]
-        )
 
-        def project(grouped, name, bank):
-            codes, scales, quantise_tiles = quantise_weight(nc, keep, grouped, name)
-            acc = psum.tile([P, PACK, ROWS], F32, tag=bank, name=name + "_acc")
-            return acc, codes, scales, quantise_tiles
+        def new_weight(name):
+            grouped = keep.tile([P, PACK * C], BF16, name=name + "_grouped", align_bytes=64)
+            codes = keep.tile([P, C], U32, name=name + "_codes", align_bytes=64)
+            scales = keep.tile([P, C], U8, name=name + "_scales", align_bytes=64)
+            return grouped, codes, scales
 
-        def project_half(projection, h):
-            acc, codes, scales, quantise_tiles = projection
-            t0, t1 = h * PACK // 2, (h + 1) * PACK // 2
-            quantise_tiles(t0, t1)
-            for t in range(t0, t1):
-                cols = slice(t * P, (t + 1) * P)
-                for first in (0, ROWS // 2):
-                    rows = slice(first, first + ROWS)
-                    nc.tensor.matmul_mx(
-                        out=acc[:, t, :],
-                        lhsT=codes[:, cols].bitcast(FP8X4),
-                        lhsT_scale=scales[:, cols],
-                        rhs=x_codes[:, rows].bitcast(FP8X4),
-                        rhs_scale=x_scales[:, rows],
-                        start=first == 0,
-                        stop=first > 0,
-                    )
-
-        def sum_over_time(total, acc, b0, b1):
-            n0, n1 = b0 * V, b1 * V
-            nc.vector.tensor_reduce(
-                out=total[:, n0:n1],
-                in_=acc[:, :, 0 : ROWS // 2].rearrange("q t (s n) -> q n t s", s=T // 2)[:, n0:n1],
-                axis=mybir.AxisListType.X,
-                op=ALU.add,
+        def regroup(copy, raw, grouped, c0, c1):
+            copy(
+                out=grouped[:, c0 * PACK : c1 * PACK].rearrange("p (c i j) -> p c j i", i=4, j=PACK),
+                in_=raw[:, :, c0:c1].rearrange("p j (c i) -> p c j i", i=4),
             )
 
-        phi_projection = project(phi_grouped, "phi", "bank5")
-        project_half(phi_projection, 0)
-        theta_grouped = regroup_weight(nc, keep, theta_raw, "theta", THETA_VECTOR_GROUPS)
-        theta_projection = project(theta_grouped, "theta", "bank6")
-        project_half(phi_projection, 1)
-        project_half(theta_projection, 0)
-        project_half(theta_projection, 1)
+        def quantise(weight, c0, c1):
+            grouped, codes, scales = weight
+            nc.vector.quantize_mx(
+                out=codes[:, c0:c1].bitcast(FP8X4),
+                scales=scales[:, c0:c1],
+                in_=grouped[:, c0 * PACK : c1 * PACK],
+            )
 
-        kappa_grouped = regroup_weight(nc, keep, kappa_raw, "kappa", 0)
+        phi, theta, kappa = new_weight("phi"), new_weight("theta"), new_weight("kappa")
+        acc_phi = psum.tile([P, PACK, ROWS], F32, tag="bank5", name="acc_phi")
+        acc_theta = psum.tile([P, PACK, ROWS], F32, tag="bank6", name="acc_theta")
 
-        phi_sum = keep.tile([P, B * V, PACK], F32)
-        sum_over_time(phi_sum, phi_projection[0], 0, B)
-        phi_biased = keep.tile([P, B * V, PACK], F32)
+        def project(acc, weight, t0, t1):
+            for t in range(t0, t1):
+                cols = slice(t * P, (t + 1) * P)
+                for s in range(T):
+                    rows = slice(s * STEP, s * STEP + ROWS)
+                    nc.tensor.matmul_mx(
+                        out=acc[:, t, :],
+                        lhsT=weight[1][:, cols].bitcast(FP8X4),
+                        lhsT_scale=weight[2][:, cols],
+                        rhs=x_codes[:, rows].bitcast(FP8X4),
+                        rhs_scale=x_scales[:, rows],
+                        start=s == 0,
+                        stop=s == T - 1,
+                    )
+
+        vcopy, scopy = nc.vector.tensor_copy, nc.scalar.copy
+        regroup(scopy, phi_raw, phi[0], PHI_VECTOR, C)
+        regroup(vcopy, phi_raw, phi[0], 0, 256)
+        regroup(vcopy, phi_raw, phi[0], 256, PHI_VECTOR)
+        nc.vector.quantize_mx(
+            out=x_codes[:, 0 : T * STEP].bitcast(FP8X4), scales=x_scales[:, 0 : T * STEP], in_=x_grouped[:]
+        )
+        quantise(phi, 0, 256)
+        project(acc_phi, phi, 0, 2)
+        regroup(scopy, theta_raw, theta[0], THETA_VECTOR, C)
+        quantise(phi, 256, C)
+        project(acc_phi, phi, 2, 4)
+        vec_ps = psum.tile([P, P], BF16, tag="bank1", name="vec_ps")
+        nc.tensor.transpose(vec_ps[:], vec_rows[:], ident_bf[:])
+        vec_t = keep.tile([P, 3 * PACK], F32, name="vec_t")
+        regroup(vcopy, theta_raw, theta[0], 0, THETA_VECTOR)
+        quantise(theta, 0, 256)
+        project(acc_theta, theta, 0, 2)
+        nc.vector.tensor_copy(out=vec_t[:], in_=vec_ps[:, 0 : 3 * PACK])
+        quantise(theta, 256, 384)
+        project(acc_theta, theta, 2, 3)
+        quantise(theta, 384, C)
+        project(acc_theta, theta, 3, 4)
+
+        regroup(scopy, kappa_raw, kappa[0], KAPPA_VECTOR, C)
+        bias_diff = keep.tile([P, PACK], F32, name="bias_diff")
+        nc.gpsimd.tensor_tensor(out=bias_diff[:], in0=vec_t[:, 0:4], in1=vec_t[:, 4:8], op=ALU.subtract)
+        lam_f = keep.tile([P, 1], F32, name="lam_f")
+        nc.gpsimd.tensor_copy(out=lam_f[:], in_=lam_bf[:])
+        lam_kappa_b = keep.tile([P, PACK], F32, name="lam_kappa_b")
+        nc.gpsimd.tensor_scalar(
+            out=lam_kappa_b[:], in0=vec_t[:, 8:12], scalar1=lam_f[:, 0:1], scalar2=None, op0=ALU.mult
+        )
+        regroup(vcopy, kappa_raw, kappa[0], 0, KAPPA_VECTOR)
+
+        phi_sum = acc_phi[:].rearrange("q t n -> q n t")
+        theta_sum = acc_theta[:].rearrange("q t n -> q n t")
+        phi_biased = keep.tile([P, B * V, PACK], F32, name="phi_biased")
         nc.vector.scalar_tensor_tensor(
             out=phi_biased[:],
             in0=bias_diff[:].unsqueeze(1).to_broadcast([P, B * V, PACK]),
             scalar=float(T),
-            in1=phi_sum[:],
+            in1=phi_sum[:, 0 : B * V],
             op0=ALU.mult,
             op1=ALU.add,
         )
-        theta_sum = keep.tile([P, B * V, PACK], F32)
-        for b in range(B):
-            sum_over_time(theta_sum, theta_projection[0], b, b + 1)
 
-        diff = keep.tile([P, B, V, V, PACK], F32)
-        f_bf = keep.tile([P, B, V, V, PACK], BF16, align_bytes=64)
-        f_codes = keep.tile([P, B, PAIRS], U32, align_bytes=64)
-        f_scales = keep.tile([P, B, PAIRS], U8, align_bytes=64)
+        idle = psum.tile([P, C], F32, tag="bank0", name="idle")
+        for i in range(IDLE_PASSES):
+            nc.tensor.matmul_mx(
+                out=idle[:],
+                lhsT=phi[1][:, 0:P].bitcast(FP8X4),
+                lhsT_scale=phi[2][:, 0:P],
+                rhs=theta[1][:].bitcast(FP8X4),
+                rhs_scale=theta[2][:],
+                start=True,
+                stop=True,
+            )
 
-        def difference_and_tanh(b, u0, u1):
+        diff = keep.tile([P, B, V, V, PACK], F32, name="diff")
+        f_bf = keep.tile([P, B, V, V, PACK], BF16, name="f_bf", align_bytes=64)
+        f_codes = keep.tile([P, B, PAIRS], U32, name="f_codes", align_bytes=64)
+        f_scales = keep.tile([P, B, PAIRS], U8, name="f_scales", align_bytes=64)
+
+        def difference(b, u0, u1):
             us = slice(u0, u1)
             nc.vector.tensor_tensor(
                 out=diff[:, b, us],
@@ -195,6 +199,20 @@ def tile_attgcn_pa_s_kernel(
                 in1=theta_sum[:, b * V : (b + 1) * V].unsqueeze(1).to_broadcast([P, u1 - u0, V, PACK]),
                 op=ALU.subtract,
             )
+
+        theta_sb = keep.tile([P, V, PACK], F32, name="theta_sb")
+        nc.scalar.copy(out=theta_sb[:], in_=theta_sum[:, V : 2 * V])
+
+        def difference_on_gpsimd(u0, u1):
+            nc.gpsimd.tensor_tensor(
+                out=diff[:, 1, u0:u1],
+                in0=phi_biased[:, V + u0 : V + u1].unsqueeze(2).to_broadcast([P, u1 - u0, V, PACK]),
+                in1=theta_sb[:].unsqueeze(1).to_broadcast([P, u1 - u0, V, PACK]),
+                op=ALU.subtract,
+            )
+
+        def tanh(b, u0, u1):
+            us = slice(u0, u1)
             nc.scalar.activation(
                 out=f_bf[:, b, us].rearrange("q u v t -> q (u v t)"),
                 in_=diff[:, b, us].rearrange("q u v t -> q (u v t)"),
@@ -210,67 +228,101 @@ def tile_attgcn_pa_s_kernel(
                 in_=f_bf[:, b, u0:u1].rearrange("q u v t -> q (u v t)"),
             )
 
-        out_sb = keep.tile([P, B, PACK, PAIRS], F32)
-        out_view = out.rearrange("b (q m) u v -> b q m (u v)", m=PACK)
+        out_sb = keep.tile([P, B, PACK, PAIRS], F32, name="out_sb")
+        out_view = out.rearrange("b (m q) u v -> b q m (u v)", m=PACK)
+        g = {}
 
-        def finish(b, m):
+        def multiply(b, m):
             cols = slice(m * P, (m + 1) * P)
-            g = psum.tile([P, PAIRS], F32, tag="bank%d" % (b * PACK + m), name="g%d%d" % (b, m))
+            tile = psum.tile([P, PAIRS], F32, tag="bank%d" % (b * PACK + m), name="g%d%d" % (b, m))
+            g[b, m] = tile
             nc.tensor.matmul_mx(
-                out=g[:],
-                lhsT=kappa_codes[:, cols].bitcast(FP8X4),
-                lhsT_scale=kappa_scales[:, cols],
+                out=tile[:],
+                lhsT=kappa[1][:, cols].bitcast(FP8X4),
+                lhsT_scale=kappa[2][:, cols],
                 rhs=f_codes[:, b, :].bitcast(FP8X4),
                 rhs_scale=f_scales[:, b, :],
                 start=True,
                 stop=True,
             )
-            nc.vector.scalar_tensor_tensor(
-                out=out_sb[:, b, m, :],
-                in0=g[:],
-                scalar=lam_f[:, 0:1],
-                in1=a_plus[:, m, :],
-                op0=ALU.mult,
-                op1=ALU.add,
-            )
+
+        def store(b, m):
             nc.sync.dma_start(out=out_view[b, :, m, :], in_=out_sb[:, b, m, :])
 
-        idle = psum.tile([P, C], F32, tag="bank0", name="idle")
-        for i in range(IDLE_PASSES):
-            nc.tensor.matmul_mx(
-                out=idle[:],
-                lhsT=phi_projection[1][:, 0:P].bitcast(FP8X4),
-                lhsT_scale=phi_projection[2][:, 0:P],
-                rhs=theta_projection[1][:].bitcast(FP8X4),
-                rhs_scale=theta_projection[2][:],
-                start=True,
-                stop=True,
-            )
-
-        a_plus = keep.tile([P, PACK, PAIRS], F32)
+        a_plus = keep.tile([P, PACK, PAIRS], F32, name="a_plus")
 
         def add_bias_to_a(m):
             nc.scalar.activation(
                 out=a_plus[:, m, :], in_=a_bf[:, m, :], func=ACT.Identity, bias=lam_kappa_b[:, m : m + 1]
             )
 
-        kappa_codes, kappa_scales, quantise_kappa = quantise_weight(nc, keep, kappa_grouped, "kappa")
+        def add_bias_to_a_on_gpsimd(m):
+            nc.gpsimd.tensor_scalar(
+                out=a_plus[:, m, :],
+                in0=a_bf[:, m, :],
+                scalar1=1.0,
+                scalar2=lam_kappa_b[:, m : m + 1],
+                op0=ALU.mult,
+                op1=ALU.add,
+            )
+
+        def finish(b, m):
+            nc.vector.scalar_tensor_tensor(
+                out=out_sb[:, b, m, :],
+                in0=g[b, m][:],
+                scalar=lam_f[:, 0:1],
+                in1=a_plus[:, m, :],
+                op0=ALU.mult,
+                op1=ALU.add,
+            )
+            store(b, m)
+
+        scaled = keep.tile([P, B, PACK, PAIRS], F32, name="scaled")
+
+        def scale_on_scalar(b, m):
+            nc.scalar.activation(
+                out=scaled[:, b, m, :],
+                in_=g[b, m][:],
+                func=ACT.Identity,
+                scale=lam_f[:, 0:1],
+                bias=lam_kappa_b[:, m : m + 1],
+            )
+
+        def add_on_gpsimd(b, m):
+            nc.gpsimd.tensor_tensor(
+                out=out_sb[:, b, m, :], in0=scaled[:, b, m, :], in1=a_bf[:, m, :], op=ALU.add
+            )
+            store(b, m)
+
         add_bias_to_a(0)
-        add_bias_to_a(1)
-        difference_and_tanh(0, 0, 8)
-        difference_and_tanh(0, 8, 16)
-        difference_and_tanh(1, 0, 8)
-        quantise_kappa(0, PACK)
+        difference(0, 0, 4)
+        tanh(0, 0, 4)
+        difference(0, 4, 8)
+        tanh(0, 4, 8)
+        difference_on_gpsimd(8, 16)
+        difference(0, 8, 16)
+        tanh(0, 8, 16)
+        difference(1, 0, 8)
+        tanh(1, 0, 8)
+        quantise(kappa, 0, 256)
         quantise_f(0, 0, V)
+        quantise(kappa, 256, C)
+        add_bias_to_a_on_gpsimd(1)
+        tanh(1, 8, 16)
         add_bias_to_a(2)
-        difference_and_tanh(1, 8, 12)
-        difference_and_tanh(1, 12, 16)
-        add_bias_to_a(3)
-        quantise_f(1, 0, 8)
-        finish(0, 0)
-        finish(0, 1)
-        quantise_f(1, 8, 16)
-        finish(0, 2)
-        finish(0, 3)
         for m in range(PACK):
-            finish(1, m)
+            multiply(0, m)
+        finish(0, 0)
+        quantise_f(1, 0, V)
+        finish(0, 1)
+        multiply(1, 3)
+        for m in range(3):
+            multiply(1, m)
+        scale_on_scalar(0, 3)
+        finish(0, 2)
+        scale_on_scalar(1, 3)
+        add_on_gpsimd(0, 3)
+        finish(1, 0)
+        finish(1, 1)
+        add_on_gpsimd(1, 3)
+        finish(1, 2)

@@ -20,7 +20,7 @@ STEP = 64
 
 PHI_VECTOR = 320
 THETA_VECTOR = 256
-KAPPA_VECTOR = 192
+KAPPA_VECTOR = 128
 IDLE_PASSES = 9
 
 FLOPS = 2 * ROWS * C * C * 2 + 2 * B * PAIRS * C * C
@@ -40,7 +40,8 @@ def tile_attgcn_pa_s_kernel(
         x_sb = keep.tile([P, C], BF16, name="x_sb")
         nc.sync.dma_start(out=x_sb[:], in_=x.rearrange("b s v f -> (b s v) f"))
         phi_raw = keep.tile([P, PACK, C], BF16, name="phi_raw")
-        nc.sync.dma_start(out=phi_raw[:], in_=phi_w.rearrange("(p j) c -> p j c", j=PACK))
+        for cols in (slice(0, 256), slice(256, C)):
+            nc.sync.dma_start(out=phi_raw[:, :, cols], in_=phi_w.rearrange("(p j) c -> p j c", j=PACK)[:, :, cols])
         theta_raw = keep.tile([P, PACK, C], BF16, name="theta_raw")
         nc.sync.dma_start(out=theta_raw[:], in_=theta_w.rearrange("(p j) c -> p j c", j=PACK))
         for i, vec in enumerate((phi_b, theta_b, kappa_b)):
@@ -67,8 +68,9 @@ def tile_attgcn_pa_s_kernel(
 
         ident = keep.tile([P, P], F32, name="ident")
         make_identity(nc, ident[:])
-        ident_bf = keep.tile([P, P], BF16, name="ident_bf")
-        nc.vector.tensor_copy(out=ident_bf[:], in_=ident[:])
+        coef = keep.tile([P, 2 * PACK], BF16, name="coef")
+        nc.vector.tensor_tensor(out=coef[:, 0:4], in0=ident[:, 0:4], in1=ident[:, 4:8], op=ALU.subtract)
+        nc.vector.tensor_copy(out=coef[:, 4:8], in_=ident[:, 8:12])
 
         early = psum.tile([P, P], F32, tag="bank0", name="early")
 
@@ -82,7 +84,7 @@ def tile_attgcn_pa_s_kernel(
         x_t = psum.tile([P, 2, ROWS], F32, tag="bank7", name="x_t")
         for h in range(2):
             nc.tensor.transpose(x_t[:, h, :], x_words[:, h, :], ident[:])
-        warm(6)
+        warm(3)
         x_dst = x_grouped[:].bitcast(F32).rearrange("q (s b v h) -> q b s v h", b=STEP // V, v=V, s=T)
         x_src = x_t[:].rearrange("q h (b s v) -> q b s v h", b=B, s=T)
         for b in range(B):
@@ -137,28 +139,29 @@ def tile_attgcn_pa_s_kernel(
         quantise(phi, 0, 256)
         project(acc_phi, phi, 0, 2)
         regroup(scopy, theta_raw, theta[0], THETA_VECTOR, C)
+        regroup(vcopy, theta_raw, theta[0], 0, 128)
         quantise(phi, 256, C)
         project(acc_phi, phi, 2, 4)
-        vec_ps = psum.tile([P, P], BF16, tag="bank1", name="vec_ps")
-        nc.tensor.transpose(vec_ps[:], vec_rows[:], ident_bf[:])
-        vec_t = keep.tile([P, 3 * PACK], F32, name="vec_t")
-        regroup(vcopy, theta_raw, theta[0], 0, THETA_VECTOR)
-        quantise(theta, 0, 256)
-        project(acc_theta, theta, 0, 2)
-        nc.vector.tensor_copy(out=vec_t[:], in_=vec_ps[:, 0 : 3 * PACK])
+        vec_ps = psum.tile([P, 2 * PACK], F32, tag="bank1", name="vec_ps")
+        nc.tensor.matmul(vec_ps[:], lhsT=vec_rows[:], rhs=coef[:], start=True, stop=True)
+        vec_t = keep.tile([P, 2 * PACK], F32, name="vec_t")
+        regroup(vcopy, theta_raw, theta[0], 128, THETA_VECTOR)
+        quantise(theta, 0, 128)
+        project(acc_theta, theta, 0, 1)
+        quantise(theta, 128, 256)
+        project(acc_theta, theta, 1, 2)
         quantise(theta, 256, 384)
         project(acc_theta, theta, 2, 3)
         quantise(theta, 384, C)
         project(acc_theta, theta, 3, 4)
 
         regroup(scopy, kappa_raw, kappa[0], KAPPA_VECTOR, C)
-        bias_diff = keep.tile([P, PACK], F32, name="bias_diff")
-        nc.gpsimd.tensor_tensor(out=bias_diff[:], in0=vec_t[:, 0:4], in1=vec_t[:, 4:8], op=ALU.subtract)
+        nc.vector.tensor_copy(out=vec_t[:], in_=vec_ps[:])
         lam_f = keep.tile([P, 1], F32, name="lam_f")
         nc.gpsimd.tensor_copy(out=lam_f[:], in_=lam_bf[:])
         lam_kappa_b = keep.tile([P, PACK], F32, name="lam_kappa_b")
         nc.gpsimd.tensor_scalar(
-            out=lam_kappa_b[:], in0=vec_t[:, 8:12], scalar1=lam_f[:, 0:1], scalar2=None, op0=ALU.mult
+            out=lam_kappa_b[:], in0=vec_t[:, 4:8], scalar1=lam_f[:, 0:1], scalar2=None, op0=ALU.mult
         )
         regroup(vcopy, kappa_raw, kappa[0], 0, KAPPA_VECTOR)
 
@@ -167,7 +170,7 @@ def tile_attgcn_pa_s_kernel(
         phi_biased = keep.tile([P, B * V, PACK], F32, name="phi_biased")
         nc.vector.scalar_tensor_tensor(
             out=phi_biased[:],
-            in0=bias_diff[:].unsqueeze(1).to_broadcast([P, B * V, PACK]),
+            in0=vec_t[:, 0:PACK].unsqueeze(1).to_broadcast([P, B * V, PACK]),
             scalar=float(T),
             in1=phi_sum[:, 0 : B * V],
             op0=ALU.mult,
@@ -201,7 +204,7 @@ def tile_attgcn_pa_s_kernel(
             )
 
         theta_sb = keep.tile([P, V, PACK], F32, name="theta_sb")
-        nc.scalar.copy(out=theta_sb[:], in_=theta_sum[:, V : 2 * V])
+        nc.vector.tensor_copy(out=theta_sb[:], in_=theta_sum[:, V : 2 * V])
 
         def difference_on_gpsimd(u0, u1):
             nc.gpsimd.tensor_tensor(

@@ -203,17 +203,6 @@ def tile_attgcn_pa_s_kernel(
                 op=ALU.subtract,
             )
 
-        theta_sb = keep.tile([P, V, PACK], F32, name="theta_sb")
-        nc.vector.tensor_copy(out=theta_sb[:], in_=theta_sum[:, V : 2 * V])
-
-        def difference_on_gpsimd(u0, u1):
-            nc.gpsimd.tensor_tensor(
-                out=diff[:, 1, u0:u1],
-                in0=phi_biased[:, V + u0 : V + u1].unsqueeze(2).to_broadcast([P, u1 - u0, V, PACK]),
-                in1=theta_sb[:].unsqueeze(1).to_broadcast([P, u1 - u0, V, PACK]),
-                op=ALU.subtract,
-            )
-
         def tanh(b, u0, u1):
             us = slice(u0, u1)
             nc.scalar.activation(
@@ -259,16 +248,6 @@ def tile_attgcn_pa_s_kernel(
                 out=a_plus[:, m, :], in_=a_bf[:, m, :], func=ACT.Identity, bias=lam_kappa_b[:, m : m + 1]
             )
 
-        def add_bias_to_a_on_gpsimd(m):
-            nc.gpsimd.tensor_scalar(
-                out=a_plus[:, m, :],
-                in0=a_bf[:, m, :],
-                scalar1=1.0,
-                scalar2=lam_kappa_b[:, m : m + 1],
-                op0=ALU.mult,
-                op1=ALU.add,
-            )
-
         def finish(b, m):
             nc.vector.scalar_tensor_tensor(
                 out=out_sb[:, b, m, :],
@@ -280,52 +259,31 @@ def tile_attgcn_pa_s_kernel(
             )
             store(b, m)
 
-        scaled = keep.tile([P, B, PACK, PAIRS], F32, name="scaled")
-
-        def scale_on_scalar(b, m):
-            nc.scalar.activation(
-                out=scaled[:, b, m, :],
-                in_=g[b, m][:],
-                func=ACT.Identity,
-                scale=lam_f[:, 0:1],
-                bias=lam_kappa_b[:, m : m + 1],
-            )
-
-        def add_on_gpsimd(b, m):
-            nc.gpsimd.tensor_tensor(
-                out=out_sb[:, b, m, :], in0=scaled[:, b, m, :], in1=a_bf[:, m, :], op=ALU.add
-            )
-            store(b, m)
+        def results(b, m):
+            multiply(b, m)
+            finish(b, m)
 
         add_bias_to_a(0)
-        difference(0, 0, 4)
-        tanh(0, 0, 4)
-        difference(0, 4, 8)
-        tanh(0, 4, 8)
-        difference_on_gpsimd(8, 16)
+        add_bias_to_a(1)
+        difference(0, 0, 8)
+        tanh(0, 0, 8)
         difference(0, 8, 16)
         tanh(0, 8, 16)
         difference(1, 0, 8)
         tanh(1, 0, 8)
-        quantise(kappa, 0, 256)
+        quantise(kappa, 0, C)
         quantise_f(0, 0, V)
-        quantise(kappa, 256, C)
-        add_bias_to_a_on_gpsimd(1)
-        tanh(1, 8, 16)
         add_bias_to_a(2)
+        difference(1, 8, 12)
+        tanh(1, 8, 12)
+        difference(1, 12, 16)
+        tanh(1, 12, 16)
+        add_bias_to_a(3)
+        quantise_f(1, 0, 8)
+        results(0, 0)
+        results(0, 1)
+        quantise_f(1, 8, 16)
+        results(0, 2)
+        results(0, 3)
         for m in range(PACK):
-            multiply(0, m)
-        finish(0, 0)
-        quantise_f(1, 0, V)
-        finish(0, 1)
-        multiply(1, 3)
-        for m in range(3):
-            multiply(1, m)
-        scale_on_scalar(0, 3)
-        finish(0, 2)
-        scale_on_scalar(1, 3)
-        add_on_gpsimd(0, 3)
-        finish(1, 0)
-        finish(1, 1)
-        add_on_gpsimd(1, 3)
-        finish(1, 2)
+            results(1, m)

@@ -22,6 +22,8 @@ PHI_VECTOR = 320
 THETA_VECTOR = 256
 KAPPA_VECTOR = 128
 IDLE_PASSES = 9
+PHI_WINDOWS = (0, 2)
+THETA_WINDOWS = (0, 1, 2, 3)
 
 FLOPS = 2 * ROWS * C * C * 2 + 2 * B * PAIRS * C * C
 
@@ -40,8 +42,7 @@ def tile_attgcn_pa_s_kernel(
         x_sb = keep.tile([P, C], BF16, name="x_sb")
         nc.sync.dma_start(out=x_sb[:], in_=x.rearrange("b s v f -> (b s v) f"))
         phi_raw = keep.tile([P, PACK, C], BF16, name="phi_raw")
-        for cols in (slice(0, 256), slice(256, C)):
-            nc.sync.dma_start(out=phi_raw[:, :, cols], in_=phi_w.rearrange("(p j) c -> p j c", j=PACK)[:, :, cols])
+        nc.sync.dma_start(out=phi_raw[:], in_=phi_w.rearrange("(p j) c -> p j c", j=PACK))
         theta_raw = keep.tile([P, PACK, C], BF16, name="theta_raw")
         nc.sync.dma_start(out=theta_raw[:], in_=theta_w.rearrange("(p j) c -> p j c", j=PACK))
         for i, vec in enumerate((phi_b, theta_b, kappa_b)):
@@ -84,7 +85,7 @@ def tile_attgcn_pa_s_kernel(
         x_t = psum.tile([P, 2, ROWS], F32, tag="bank7", name="x_t")
         for h in range(2):
             nc.tensor.transpose(x_t[:, h, :], x_words[:, h, :], ident[:])
-        warm(3)
+        warm(6)
         x_dst = x_grouped[:].bitcast(F32).rearrange("q (s b v h) -> q b s v h", b=STEP // V, v=V, s=T)
         x_src = x_t[:].rearrange("q h (b s v) -> q b s v h", b=B, s=T)
         for b in range(B):
@@ -114,19 +115,19 @@ def tile_attgcn_pa_s_kernel(
         acc_phi = psum.tile([P, PACK, ROWS], F32, tag="bank5", name="acc_phi")
         acc_theta = psum.tile([P, PACK, ROWS], F32, tag="bank6", name="acc_theta")
 
-        def project(acc, weight, t0, t1):
+        def project(acc, weight, t0, t1, windows):
             for t in range(t0, t1):
                 cols = slice(t * P, (t + 1) * P)
-                for s in range(T):
-                    rows = slice(s * STEP, s * STEP + ROWS)
+                for w in windows:
+                    rows = slice(w * STEP, w * STEP + ROWS)
                     nc.tensor.matmul_mx(
                         out=acc[:, t, :],
                         lhsT=weight[1][:, cols].bitcast(FP8X4),
                         lhsT_scale=weight[2][:, cols],
                         rhs=x_codes[:, rows].bitcast(FP8X4),
                         rhs_scale=x_scales[:, rows],
-                        start=s == 0,
-                        stop=s == T - 1,
+                        start=w == windows[0],
+                        stop=w == windows[-1],
                     )
 
         vcopy, scopy = nc.vector.tensor_copy, nc.scalar.copy
@@ -137,23 +138,23 @@ def tile_attgcn_pa_s_kernel(
             out=x_codes[:, 0 : T * STEP].bitcast(FP8X4), scales=x_scales[:, 0 : T * STEP], in_=x_grouped[:]
         )
         quantise(phi, 0, 256)
-        project(acc_phi, phi, 0, 2)
+        project(acc_phi, phi, 0, 2, PHI_WINDOWS)
         regroup(scopy, theta_raw, theta[0], THETA_VECTOR, C)
         regroup(vcopy, theta_raw, theta[0], 0, 128)
         quantise(phi, 256, C)
-        project(acc_phi, phi, 2, 4)
+        project(acc_phi, phi, 2, 4, PHI_WINDOWS)
         vec_ps = psum.tile([P, 2 * PACK], F32, tag="bank1", name="vec_ps")
         nc.tensor.matmul(vec_ps[:], lhsT=vec_rows[:], rhs=coef[:], start=True, stop=True)
         vec_t = keep.tile([P, 2 * PACK], F32, name="vec_t")
         regroup(vcopy, theta_raw, theta[0], 128, THETA_VECTOR)
         quantise(theta, 0, 128)
-        project(acc_theta, theta, 0, 1)
+        project(acc_theta, theta, 0, 1, THETA_WINDOWS)
         quantise(theta, 128, 256)
-        project(acc_theta, theta, 1, 2)
+        project(acc_theta, theta, 1, 2, THETA_WINDOWS)
         quantise(theta, 256, 384)
-        project(acc_theta, theta, 2, 3)
+        project(acc_theta, theta, 2, 3, THETA_WINDOWS)
         quantise(theta, 384, C)
-        project(acc_theta, theta, 3, 4)
+        project(acc_theta, theta, 3, 4, THETA_WINDOWS)
 
         regroup(scopy, kappa_raw, kappa[0], KAPPA_VECTOR, C)
         nc.vector.tensor_copy(out=vec_t[:], in_=vec_ps[:])
@@ -163,19 +164,22 @@ def tile_attgcn_pa_s_kernel(
         nc.gpsimd.tensor_scalar(
             out=lam_kappa_b[:], in0=vec_t[:, 4:8], scalar1=lam_f[:, 0:1], scalar2=None, op0=ALU.mult
         )
-        regroup(vcopy, kappa_raw, kappa[0], 0, KAPPA_VECTOR)
 
         phi_sum = acc_phi[:].rearrange("q t n -> q n t")
         theta_sum = acc_theta[:].rearrange("q t n -> q n t")
-        phi_biased = keep.tile([P, B * V, PACK], F32, name="phi_biased")
+        phi_part = keep.tile([P, B * V, PACK], F32, name="phi_part")
         nc.vector.scalar_tensor_tensor(
-            out=phi_biased[:],
+            out=phi_part[:],
             in0=vec_t[:, 0:PACK].unsqueeze(1).to_broadcast([P, B * V, PACK]),
             scalar=float(T),
             in1=phi_sum[:, 0 : B * V],
             op0=ALU.mult,
             op1=ALU.add,
         )
+
+        regroup(vcopy, kappa_raw, kappa[0], 0, KAPPA_VECTOR)
+        phi_biased = keep.tile([P, B * V, PACK], F32, name="phi_biased")
+        nc.vector.tensor_tensor(out=phi_biased[:], in0=phi_part[:], in1=phi_sum[:, STEP : STEP + B * V], op=ALU.add)
 
         idle = psum.tile([P, C], F32, tag="bank0", name="idle")
         for i in range(IDLE_PASSES):

@@ -20,7 +20,7 @@ STEP = 64
 
 PHI_VECTOR = 320
 THETA_VECTOR = 256
-KAPPA_VECTOR = 128
+KAPPA_VECTOR = 32
 IDLE_PASSES = 9
 PHI_WINDOWS = (0, 2)
 THETA_WINDOWS = (0, 1, 2, 3)
@@ -45,14 +45,16 @@ def tile_attgcn_pa_s_kernel(
         nc.sync.dma_start(out=phi_raw[:], in_=phi_w.rearrange("(p j) c -> p j c", j=PACK))
         theta_raw = keep.tile([P, PACK, C], BF16, name="theta_raw")
         nc.sync.dma_start(out=theta_raw[:], in_=theta_w.rearrange("(p j) c -> p j c", j=PACK))
-        for i, vec in enumerate((phi_b, theta_b, kappa_b)):
+        for i, vec in enumerate((phi_b, theta_b)):
             nc.sync.dma_start(out=vec_rows[PACK * i : PACK * (i + 1), :], in_=vec.rearrange("(t q) -> t q", t=PACK))
         kappa_raw = keep.tile([P, PACK, C], BF16, name="kappa_raw")
         nc.sync.dma_start(out=kappa_raw[:], in_=kappa_w.rearrange("(j p) c -> p j c", j=PACK))
+        kappa_b_bf = keep.tile([P, PACK], BF16, name="kappa_b_bf")
+        nc.sync.dma_start(out=kappa_b_bf[:], in_=kappa_b.rearrange("(q m) -> q m", m=PACK))
         lam_bf = keep.tile([P, 1], BF16, name="lam_bf")
         nc.sync.dma_start(out=lam_bf[:], in_=lam.partition_broadcast(P))
         a_bf = keep.tile([P, PACK, PAIRS], BF16, name="a_bf")
-        nc.sync.dma_start(out=a_bf[:], in_=A.rearrange("(m q) u v -> q m (u v)", m=PACK))
+        nc.sync.dma_start(out=a_bf[:], in_=A.rearrange("(q m) u v -> q m (u v)", m=PACK))
 
         x_codes = keep.tile([P, (T + 1) * STEP], U32, name="x_codes", align_bytes=64)
         x_scales = keep.tile([P, (T + 1) * STEP], U8, name="x_scales", align_bytes=64)
@@ -69,9 +71,8 @@ def tile_attgcn_pa_s_kernel(
 
         ident = keep.tile([P, P], F32, name="ident")
         make_identity(nc, ident[:])
-        coef = keep.tile([P, 2 * PACK], BF16, name="coef")
-        nc.vector.tensor_tensor(out=coef[:, 0:4], in0=ident[:, 0:4], in1=ident[:, 4:8], op=ALU.subtract)
-        nc.vector.tensor_copy(out=coef[:, 4:8], in_=ident[:, 8:12])
+        coef = keep.tile([P, PACK], BF16, name="coef")
+        nc.vector.tensor_tensor(out=coef[:], in0=ident[:, 0:4], in1=ident[:, 4:8], op=ALU.subtract)
 
         early = psum.tile([P, P], F32, tag="bank0", name="early")
 
@@ -101,6 +102,12 @@ def tile_attgcn_pa_s_kernel(
             copy(
                 out=grouped[:, c0 * PACK : c1 * PACK].rearrange("p (c i j) -> p c j i", i=4, j=PACK),
                 in_=raw[:, :, c0:c1].rearrange("p j (c i) -> p c j i", i=4),
+            )
+
+        def regroup_kappa(copy, q0, q1):
+            copy(
+                out=kappa[0][:].rearrange("p (m q j) -> p q j m", m=PACK, j=PACK)[:, q0:q1],
+                in_=kappa_raw[:].rearrange("p j (q m) -> p q j m", m=PACK)[:, q0:q1],
             )
 
         def quantise(weight, c0, c1):
@@ -143,9 +150,9 @@ def tile_attgcn_pa_s_kernel(
         regroup(vcopy, theta_raw, theta[0], 0, 128)
         quantise(phi, 256, C)
         project(acc_phi, phi, 2, 4, PHI_WINDOWS)
-        vec_ps = psum.tile([P, 2 * PACK], F32, tag="bank1", name="vec_ps")
+        vec_ps = psum.tile([P, PACK], F32, tag="bank1", name="vec_ps")
         nc.tensor.matmul(vec_ps[:], lhsT=vec_rows[:], rhs=coef[:], start=True, stop=True)
-        vec_t = keep.tile([P, 2 * PACK], F32, name="vec_t")
+        vec_t = keep.tile([P, PACK], F32, name="vec_t")
         regroup(vcopy, theta_raw, theta[0], 128, THETA_VECTOR)
         quantise(theta, 0, 128)
         project(acc_theta, theta, 0, 1, THETA_WINDOWS)
@@ -156,13 +163,13 @@ def tile_attgcn_pa_s_kernel(
         quantise(theta, 384, C)
         project(acc_theta, theta, 3, 4, THETA_WINDOWS)
 
-        regroup(scopy, kappa_raw, kappa[0], KAPPA_VECTOR, C)
+        regroup_kappa(scopy, KAPPA_VECTOR, P)
         nc.vector.tensor_copy(out=vec_t[:], in_=vec_ps[:])
         lam_f = keep.tile([P, 1], F32, name="lam_f")
         nc.gpsimd.tensor_copy(out=lam_f[:], in_=lam_bf[:])
         lam_kappa_b = keep.tile([P, PACK], F32, name="lam_kappa_b")
         nc.gpsimd.tensor_scalar(
-            out=lam_kappa_b[:], in0=vec_t[:, 4:8], scalar1=lam_f[:, 0:1], scalar2=None, op0=ALU.mult
+            out=lam_kappa_b[:], in0=kappa_b_bf[:], scalar1=lam_f[:, 0:1], scalar2=None, op0=ALU.mult
         )
 
         phi_sum = acc_phi[:].rearrange("q t n -> q n t")
@@ -177,7 +184,7 @@ def tile_attgcn_pa_s_kernel(
             op1=ALU.add,
         )
 
-        regroup(vcopy, kappa_raw, kappa[0], 0, KAPPA_VECTOR)
+        regroup_kappa(vcopy, 0, KAPPA_VECTOR)
         phi_biased = keep.tile([P, B * V, PACK], F32, name="phi_biased")
         nc.vector.tensor_tensor(out=phi_biased[:], in0=phi_part[:], in1=phi_sum[:, STEP : STEP + B * V], op=ALU.add)
 
@@ -225,7 +232,7 @@ def tile_attgcn_pa_s_kernel(
             )
 
         out_sb = keep.tile([P, B, PACK, PAIRS], F32, name="out_sb")
-        out_view = out.rearrange("b (m q) u v -> b q m (u v)", m=PACK)
+        out_view = out.rearrange("b (q m) u v -> b q m (u v)", m=PACK)
         g = {}
 
         def multiply(b, m):

@@ -18,7 +18,7 @@ ROWS = B * T * V
 PAIRS = V * V
 STEP = 64
 
-PHI_VECTOR = 320
+PHI_VECTOR = 256
 THETA_VECTOR = 256
 KAPPA_VECTOR = 32
 IDLE_PASSES = 9
@@ -86,7 +86,7 @@ def tile_attgcn_pa_s_kernel(
         x_t = psum.tile([P, 2, ROWS], F32, tag="bank7", name="x_t")
         for h in range(2):
             nc.tensor.transpose(x_t[:, h, :], x_words[:, h, :], ident[:])
-        warm(6)
+        warm(5)
         x_dst = x_grouped[:].bitcast(F32).rearrange("q (s b v h) -> q b s v h", b=STEP // V, v=V, s=T)
         x_src = x_t[:].rearrange("q h (b s v) -> q b s v h", b=B, s=T)
         for b in range(B):
@@ -140,31 +140,29 @@ def tile_attgcn_pa_s_kernel(
         vcopy, scopy = nc.vector.tensor_copy, nc.scalar.copy
         regroup(scopy, phi_raw, phi[0], PHI_VECTOR, C)
         regroup(vcopy, phi_raw, phi[0], 0, 256)
-        regroup(vcopy, phi_raw, phi[0], 256, PHI_VECTOR)
         nc.vector.quantize_mx(
             out=x_codes[:, 0 : T * STEP].bitcast(FP8X4), scales=x_scales[:, 0 : T * STEP], in_=x_grouped[:]
         )
         quantise(phi, 0, 256)
         project(acc_phi, phi, 0, 2, PHI_WINDOWS)
-        regroup(scopy, theta_raw, theta[0], THETA_VECTOR, C)
-        regroup(vcopy, theta_raw, theta[0], 0, 128)
-        quantise(phi, 256, C)
-        project(acc_phi, phi, 2, 4, PHI_WINDOWS)
         vec_ps = psum.tile([P, PACK], F32, tag="bank1", name="vec_ps")
         nc.tensor.matmul(vec_ps[:], lhsT=vec_rows[:], rhs=coef[:], start=True, stop=True)
         vec_t = keep.tile([P, PACK], F32, name="vec_t")
-        regroup(vcopy, theta_raw, theta[0], 128, THETA_VECTOR)
+        regroup(scopy, theta_raw, theta[0], THETA_VECTOR, C)
+        regroup(vcopy, theta_raw, theta[0], 0, THETA_VECTOR)
+        quantise(phi, 256, C)
+        project(acc_phi, phi, 2, 4, PHI_WINDOWS)
         quantise(theta, 0, 128)
         project(acc_theta, theta, 0, 1, THETA_WINDOWS)
         quantise(theta, 128, 256)
         project(acc_theta, theta, 1, 2, THETA_WINDOWS)
+        nc.vector.tensor_copy(out=vec_t[:], in_=vec_ps[:])
         quantise(theta, 256, 384)
         project(acc_theta, theta, 2, 3, THETA_WINDOWS)
         quantise(theta, 384, C)
         project(acc_theta, theta, 3, 4, THETA_WINDOWS)
 
         regroup_kappa(scopy, KAPPA_VECTOR, P)
-        nc.vector.tensor_copy(out=vec_t[:], in_=vec_ps[:])
         lam_f = keep.tile([P, 1], F32, name="lam_f")
         nc.gpsimd.tensor_copy(out=lam_f[:], in_=lam_bf[:])
         lam_kappa_b = keep.tile([P, PACK], F32, name="lam_kappa_b")
@@ -233,6 +231,7 @@ def tile_attgcn_pa_s_kernel(
 
         out_sb = keep.tile([P, B, PACK, PAIRS], F32, name="out_sb")
         out_view = out.rearrange("b (q m) u v -> b q m (u v)", m=PACK)
+        a_plus = keep.tile([P, PACK, PAIRS], F32, name="a_plus")
         g = {}
 
         def multiply(b, m):
@@ -252,11 +251,18 @@ def tile_attgcn_pa_s_kernel(
         def store(b, m):
             nc.sync.dma_start(out=out_view[b, :, m, :], in_=out_sb[:, b, m, :])
 
-        a_plus = keep.tile([P, PACK, PAIRS], F32, name="a_plus")
-
         def add_bias_to_a(m):
             nc.scalar.activation(
                 out=a_plus[:, m, :], in_=a_bf[:, m, :], func=ACT.Identity, bias=lam_kappa_b[:, m : m + 1]
+            )
+
+        def add_bias_to_a_on_vector(m):
+            nc.vector.tensor_scalar(
+                out=a_plus[:, m, :],
+                in0=a_bf[:, m, :],
+                scalar1=lam_kappa_b[:, m : m + 1],
+                scalar2=None,
+                op0=ALU.add,
             )
 
         def finish(b, m):
@@ -270,31 +276,35 @@ def tile_attgcn_pa_s_kernel(
             )
             store(b, m)
 
-        def results(b, m):
-            multiply(b, m)
-            finish(b, m)
-
-        add_bias_to_a(0)
-        add_bias_to_a(1)
-        difference(0, 0, 8)
-        tanh(0, 0, 8)
-        difference(0, 8, 16)
-        tanh(0, 8, 16)
+        add_bias_to_a_on_vector(0)
+        difference(0, 0, 4)
+        tanh(0, 0, 4)
+        difference(0, 4, 8)
+        tanh(0, 4, 8)
+        difference(0, 8, 12)
+        tanh(0, 8, 12)
+        difference(0, 12, 16)
+        tanh(0, 12, 16)
         difference(1, 0, 8)
         tanh(1, 0, 8)
-        quantise(kappa, 0, C)
+        quantise(kappa, 0, 256)
         quantise_f(0, 0, V)
-        add_bias_to_a(2)
+        add_bias_to_a(1)
         difference(1, 8, 12)
         tanh(1, 8, 12)
         difference(1, 12, 16)
         tanh(1, 12, 16)
-        add_bias_to_a(3)
-        quantise_f(1, 0, 8)
-        results(0, 0)
-        results(0, 1)
-        quantise_f(1, 8, 16)
-        results(0, 2)
-        results(0, 3)
+        quantise(kappa, 256, C)
         for m in range(PACK):
-            results(1, m)
+            multiply(0, m)
+        finish(0, 0)
+        finish(0, 1)
+        add_bias_to_a(2)
+        quantise_f(1, 0, V)
+        for m in range(PACK):
+            multiply(1, m)
+        add_bias_to_a(3)
+        finish(0, 2)
+        finish(0, 3)
+        for m in range(PACK):
+            finish(1, m)

from contextlib import ExitStack

import concourse.mybir as mybir
from concourse.masks import make_identity

F32 = mybir.dt.float32
BF16 = mybir.dt.bfloat16
U32 = mybir.dt.uint32
U8 = mybir.dt.uint8
FP8X4 = mybir.dt.float8_e4m3fn_x4
ALU = mybir.AluOpType
ACT = mybir.ActivationFunctionType

P = 128
PACK = 4
B, T, V, C = 2, 4, 16, 512
ROWS = B * T * V
PAIRS = V * V
STEP = 64

PHI_VECTOR = 256
THETA_VECTOR = 256
KAPPA_VECTOR = 32
IDLE_PASSES = 9
PHI_WINDOWS = (0, 2)
THETA_WINDOWS = (0, 1, 2, 3)

FLOPS = 2 * ROWS * C * C * 2 + 2 * B * PAIRS * C * C


def tile_attgcn_pa_s_kernel(
    tc, x, A, lam, phi_w, phi_b, theta_w, theta_b, kappa_w, kappa_b, out
):
    nc = tc.nc
    with ExitStack() as ctx:
        keep = ctx.enter_context(tc.tile_pool(name="keep", bufs=1))
        psum = ctx.enter_context(tc.psum_pool(name="psum", bufs=1))
        ctx.enter_context(tc.manual_schedule())

        vec_rows = keep.tile([P, P], BF16, name="vec_rows")
        nc.vector.memset(vec_rows[:].bitcast(F32), 0.0)
        x_sb = keep.tile([P, C], BF16, name="x_sb")
        nc.sync.dma_start(out=x_sb[:], in_=x.rearrange("b s v f -> (b s v) f"))
        phi_raw = keep.tile([P, PACK, C], BF16, name="phi_raw")
        nc.sync.dma_start(out=phi_raw[:], in_=phi_w.rearrange("(p j) c -> p j c", j=PACK))
        theta_raw = keep.tile([P, PACK, C], BF16, name="theta_raw")
        nc.sync.dma_start(out=theta_raw[:], in_=theta_w.rearrange("(p j) c -> p j c", j=PACK))
        for i, vec in enumerate((phi_b, theta_b)):
            nc.sync.dma_start(out=vec_rows[PACK * i : PACK * (i + 1), :], in_=vec.rearrange("(t q) -> t q", t=PACK))
        kappa_raw = keep.tile([P, PACK, C], BF16, name="kappa_raw")
        nc.sync.dma_start(out=kappa_raw[:], in_=kappa_w.rearrange("(j p) c -> p j c", j=PACK))
        kappa_b_bf = keep.tile([P, PACK], BF16, name="kappa_b_bf")
        nc.sync.dma_start(out=kappa_b_bf[:], in_=kappa_b.rearrange("(q m) -> q m", m=PACK))
        lam_bf = keep.tile([P, 1], BF16, name="lam_bf")
        nc.sync.dma_start(out=lam_bf[:], in_=lam.partition_broadcast(P))
        a_bf = keep.tile([P, PACK, PAIRS], BF16, name="a_bf")
        nc.sync.dma_start(out=a_bf[:], in_=A.rearrange("(q m) u v -> q m (u v)", m=PACK))

        x_codes = keep.tile([P, (T + 1) * STEP], U32, name="x_codes", align_bytes=64)
        x_scales = keep.tile([P, (T + 1) * STEP], U8, name="x_scales", align_bytes=64)
        nc.vector.memset(x_codes[:, T * STEP :], 0)
        nc.vector.memset(x_scales[:, T * STEP :], 0)
        x_grouped = keep.tile([P, T * STEP * PACK], BF16, name="x_grouped", align_bytes=64)
        nc.vector.memset(
            x_grouped[:].bitcast(F32).rearrange("q (s n) -> q s n", s=T)[:, :, B * V * PACK // 2 :], 0.0
        )
        warm_in = keep.tile([P, 1], F32, name="warm_in")
        nc.vector.memset(warm_in[:], 0.0)
        warm_out = keep.tile([P, 1], F32, name="warm_out")
        nc.scalar.activation(out=warm_out[:], in_=warm_in[:], func=ACT.Tanh)

        ident = keep.tile([P, P], F32, name="ident")
        make_identity(nc, ident[:])
        coef = keep.tile([P, PACK], BF16, name="coef")
        nc.vector.tensor_tensor(out=coef[:], in0=ident[:, 0:4], in1=ident[:, 4:8], op=ALU.subtract)

        early = psum.tile([P, P], F32, tag="bank0", name="early")

        def warm(passes):
            for i in range(passes):
                nc.tensor.matmul(early[:], lhsT=ident[:], rhs=ident[:], start=True, stop=True)

        warm(2)

        x_words = x_sb[:].bitcast(F32).rearrange("r (q h) -> r h q", h=2)
        x_t = psum.tile([P, 2, ROWS], F32, tag="bank7", name="x_t")
        for h in range(2):
            nc.tensor.transpose(x_t[:, h, :], x_words[:, h, :], ident[:])
        warm(5)
        x_dst = x_grouped[:].bitcast(F32).rearrange("q (s b v h) -> q b s v h", b=STEP // V, v=V, s=T)
        x_src = x_t[:].rearrange("q h (b s v) -> q b s v h", b=B, s=T)
        for b in range(B):
            nc.scalar.copy(out=x_dst[:, b], in_=x_src[:, b])

        def new_weight(name):
            grouped = keep.tile([P, PACK * C], BF16, name=name + "_grouped", align_bytes=64)
            codes = keep.tile([P, C], U32, name=name + "_codes", align_bytes=64)
            scales = keep.tile([P, C], U8, name=name + "_scales", align_bytes=64)
            return grouped, codes, scales

        def regroup(copy, raw, grouped, c0, c1):
            copy(
                out=grouped[:, c0 * PACK : c1 * PACK].rearrange("p (c i j) -> p c j i", i=4, j=PACK),
                in_=raw[:, :, c0:c1].rearrange("p j (c i) -> p c j i", i=4),
            )

        def regroup_kappa(copy, q0, q1):
            copy(
                out=kappa[0][:].rearrange("p (m q j) -> p q j m", m=PACK, j=PACK)[:, q0:q1],
                in_=kappa_raw[:].rearrange("p j (q m) -> p q j m", m=PACK)[:, q0:q1],
            )

        def quantise(weight, c0, c1):
            grouped, codes, scales = weight
            nc.vector.quantize_mx(
                out=codes[:, c0:c1].bitcast(FP8X4),
                scales=scales[:, c0:c1],
                in_=grouped[:, c0 * PACK : c1 * PACK],
            )

        phi, theta, kappa = new_weight("phi"), new_weight("theta"), new_weight("kappa")
        acc_phi = psum.tile([P, PACK, ROWS], F32, tag="bank5", name="acc_phi")
        acc_theta = psum.tile([P, PACK, ROWS], F32, tag="bank6", name="acc_theta")

        def project(acc, weight, t0, t1, windows):
            for t in range(t0, t1):
                cols = slice(t * P, (t + 1) * P)
                for w in windows:
                    rows = slice(w * STEP, w * STEP + ROWS)
                    nc.tensor.matmul_mx(
                        out=acc[:, t, :],
                        lhsT=weight[1][:, cols].bitcast(FP8X4),
                        lhsT_scale=weight[2][:, cols],
                        rhs=x_codes[:, rows].bitcast(FP8X4),
                        rhs_scale=x_scales[:, rows],
                        start=w == windows[0],
                        stop=w == windows[-1],
                    )

        vcopy, scopy = nc.vector.tensor_copy, nc.scalar.copy
        regroup(scopy, phi_raw, phi[0], PHI_VECTOR, C)
        regroup(vcopy, phi_raw, phi[0], 0, 256)
        nc.vector.quantize_mx(
            out=x_codes[:, 0 : T * STEP].bitcast(FP8X4), scales=x_scales[:, 0 : T * STEP], in_=x_grouped[:]
        )
        quantise(phi, 0, 256)
        project(acc_phi, phi, 0, 2, PHI_WINDOWS)
        vec_ps = psum.tile([P, PACK], F32, tag="bank1", name="vec_ps")
        nc.tensor.matmul(vec_ps[:], lhsT=vec_rows[:], rhs=coef[:], start=True, stop=True)
        vec_t = keep.tile([P, PACK], F32, name="vec_t")
        regroup(scopy, theta_raw, theta[0], THETA_VECTOR, C)
        regroup(vcopy, theta_raw, theta[0], 0, THETA_VECTOR)
        quantise(phi, 256, C)
        project(acc_phi, phi, 2, 4, PHI_WINDOWS)
        quantise(theta, 0, 128)
        project(acc_theta, theta, 0, 1, THETA_WINDOWS)
        quantise(theta, 128, 256)
        project(acc_theta, theta, 1, 2, THETA_WINDOWS)
        nc.vector.tensor_copy(out=vec_t[:], in_=vec_ps[:])
        quantise(theta, 256, 384)
        project(acc_theta, theta, 2, 3, THETA_WINDOWS)
        quantise(theta, 384, C)
        project(acc_theta, theta, 3, 4, THETA_WINDOWS)

        regroup_kappa(scopy, KAPPA_VECTOR, P)
        lam_f = keep.tile([P, 1], F32, name="lam_f")
        nc.gpsimd.tensor_copy(out=lam_f[:], in_=lam_bf[:])
        lam_kappa_b = keep.tile([P, PACK], F32, name="lam_kappa_b")
        nc.gpsimd.tensor_scalar(
            out=lam_kappa_b[:], in0=kappa_b_bf[:], scalar1=lam_f[:, 0:1], scalar2=None, op0=ALU.mult
        )

        phi_sum = acc_phi[:].rearrange("q t n -> q n t")
        theta_sum = acc_theta[:].rearrange("q t n -> q n t")
        phi_part = keep.tile([P, B * V, PACK], F32, name="phi_part")
        nc.vector.scalar_tensor_tensor(
            out=phi_part[:],
            in0=vec_t[:, 0:PACK].unsqueeze(1).to_broadcast([P, B * V, PACK]),
            scalar=float(T),
            in1=phi_sum[:, 0 : B * V],
            op0=ALU.mult,
            op1=ALU.add,
        )

        regroup_kappa(vcopy, 0, KAPPA_VECTOR)
        phi_biased = keep.tile([P, B * V, PACK], F32, name="phi_biased")
        nc.vector.tensor_tensor(out=phi_biased[:], in0=phi_part[:], in1=phi_sum[:, STEP : STEP + B * V], op=ALU.add)

        idle = psum.tile([P, C], F32, tag="bank0", name="idle")
        for i in range(IDLE_PASSES):
            nc.tensor.matmul_mx(
                out=idle[:],
                lhsT=phi[1][:, 0:P].bitcast(FP8X4),
                lhsT_scale=phi[2][:, 0:P],
                rhs=theta[1][:].bitcast(FP8X4),
                rhs_scale=theta[2][:],
                start=True,
                stop=True,
            )

        diff = keep.tile([P, B, V, V, PACK], F32, name="diff")
        f_bf = keep.tile([P, B, V, V, PACK], BF16, name="f_bf", align_bytes=64)
        f_codes = keep.tile([P, B, PAIRS], U32, name="f_codes", align_bytes=64)
        f_scales = keep.tile([P, B, PAIRS], U8, name="f_scales", align_bytes=64)

        def difference(b, u0, u1):
            us = slice(u0, u1)
            nc.vector.tensor_tensor(
                out=diff[:, b, us],
                in0=phi_biased[:, b * V + u0 : b * V + u1].unsqueeze(2).to_broadcast([P, u1 - u0, V, PACK]),
                in1=theta_sum[:, b * V : (b + 1) * V].unsqueeze(1).to_broadcast([P, u1 - u0, V, PACK]),
                op=ALU.subtract,
            )

        def tanh(b, u0, u1):
            us = slice(u0, u1)
            nc.scalar.activation(
                out=f_bf[:, b, us].rearrange("q u v t -> q (u v t)"),
                in_=diff[:, b, us].rearrange("q u v t -> q (u v t)"),
                func=ACT.Tanh,
                scale=1.0 / T,
            )

        def quantise_f(b, u0, u1):
            pairs = slice(u0 * V, u1 * V)
            nc.vector.quantize_mx(
                out=f_codes[:, b, pairs].bitcast(FP8X4),
                scales=f_scales[:, b, pairs],
                in_=f_bf[:, b, u0:u1].rearrange("q u v t -> q (u v t)"),
            )

        out_sb = keep.tile([P, B, PACK, PAIRS], F32, name="out_sb")
        out_view = out.rearrange("b (q m) u v -> b q m (u v)", m=PACK)
        a_plus = keep.tile([P, PACK, PAIRS], F32, name="a_plus")
        g = {}

        def multiply(b, m):
            cols = slice(m * P, (m + 1) * P)
            tile = psum.tile([P, PAIRS], F32, tag="bank%d" % (b * PACK + m), name="g%d%d" % (b, m))
            g[b, m] = tile
            nc.tensor.matmul_mx(
                out=tile[:],
                lhsT=kappa[1][:, cols].bitcast(FP8X4),
                lhsT_scale=kappa[2][:, cols],
                rhs=f_codes[:, b, :].bitcast(FP8X4),
                rhs_scale=f_scales[:, b, :],
                start=True,
                stop=True,
            )

        def store(b, m):
            nc.sync.dma_start(out=out_view[b, :, m, :], in_=out_sb[:, b, m, :])

        def add_bias_to_a(m):
            nc.scalar.activation(
                out=a_plus[:, m, :], in_=a_bf[:, m, :], func=ACT.Identity, bias=lam_kappa_b[:, m : m + 1]
            )

        def add_bias_to_a_on_vector(m):
            nc.vector.tensor_scalar(
                out=a_plus[:, m, :],
                in0=a_bf[:, m, :],
                scalar1=lam_kappa_b[:, m : m + 1],
                scalar2=None,
                op0=ALU.add,
            )

        def finish(b, m):
            nc.vector.scalar_tensor_tensor(
                out=out_sb[:, b, m, :],
                in0=g[b, m][:],
                scalar=lam_f[:, 0:1],
                in1=a_plus[:, m, :],
                op0=ALU.mult,
                op1=ALU.add,
            )
            store(b, m)

        add_bias_to_a_on_vector(0)
        difference(0, 0, 4)
        tanh(0, 0, 4)
        difference(0, 4, 8)
        tanh(0, 4, 8)
        difference(0, 8, 12)
        tanh(0, 8, 12)
        difference(0, 12, 16)
        tanh(0, 12, 16)
        difference(1, 0, 8)
        tanh(1, 0, 8)
        quantise(kappa, 0, 256)
        quantise_f(0, 0, V)
        add_bias_to_a(1)
        difference(1, 8, 12)
        tanh(1, 8, 12)
        difference(1, 12, 16)
        tanh(1, 12, 16)
        quantise(kappa, 256, C)
        for m in range(PACK):
            multiply(0, m)
        finish(0, 0)
        finish(0, 1)
        add_bias_to_a(2)
        quantise_f(1, 0, V)
        for m in range(PACK):
            multiply(1, m)
        add_bias_to_a(3)
        finish(0, 2)
        finish(0, 3)
        for m in range(PACK):
            finish(1, m)
